import numpy as np
import ml_dtypes


def mxq(x, axis, fmt="e4m3"):
    dtype, down = {"e4m3": (ml_dtypes.float8_e4m3fn, 7), "e5m2": (ml_dtypes.float8_e5m2, 14)}[fmt]
    v = np.moveaxis(np.asarray(x, np.float32).astype(ml_dtypes.bfloat16).astype(np.float64), axis, -1)
    blocks = v.reshape(v.shape[:-1] + (-1, 32))
    amax = np.abs(blocks).max(-1, keepdims=True)
    byte = np.maximum(np.where(amax > 0, np.frexp(amax)[1] - 1 + 127, 0) - down, 1)
    scale = np.exp2(byte - 127.0)
    codes = (blocks / scale).astype(np.float32).astype(dtype).astype(np.float64)
    return np.moveaxis((codes * scale).reshape(v.shape), -1, axis)


WIDE = False


def mx_kscale(k):
    if not WIDE:
        return np.ones(k)
    levels = np.array([10, -10, 5, -5, 0])
    a = np.random.permutation(np.resize(levels, k // 512 * 4)).reshape(k // 512, 4)
    idx = np.arange(k)
    return np.exp2(a[idx // 512, idx % 128 // 32])


BF16 = ml_dtypes.bfloat16


def bf(x):
    return np.asarray(x, np.float32).astype(BF16)


def f64(x):
    return np.asarray(x).astype(np.float64)


B, CIN, H, W, CK, CV, COUT, S = 1, 1024, 64, 64, 128, 512, 512, 2
HP, WP = H // S, W // S
NW, L = S * S, HP * WP


def to_windows(t):
    c = t.shape[1]
    return t.reshape(B, c, S, HP, S, WP).transpose(0, 2, 4, 3, 5, 1).reshape(B, NW, L, c)


def setup_inputs():
    s = mx_kscale(CIN)
    return {"x": bf(np.random.standard_normal((B, CIN, H, W)) * s[None, :, None, None]),
            "q": bf(np.maximum(np.random.standard_normal((B, CK, H, W)) * 2.2, 0.0)),
            "k": bf(np.maximum(np.random.standard_normal((B, CK, H, W)) * 2.2, 0.0)),
            "v_w": bf(np.random.standard_normal((CV, CIN)) * 1.5 / np.sqrt(CIN) / s[None, :]),
            "v_b": bf(np.random.standard_normal(CV) * 0.3)}


def reference(x, q, k, v_w, v_b):
    v = (mxq(f64(v_w), 1, "e4m3") @ mxq(f64(x).reshape(B, CIN, H * W), 1, "e4m3")) + f64(v_b)[None, :, None]
    qw, kw, vw = to_windows(f64(q)), to_windows(f64(k)), to_windows(v.reshape(B, CV, H, W))
    sim = qw @ kw.transpose(0, 1, 3, 2) * CK ** -0.5
    e = np.exp(sim - sim.max(-1, keepdims=True))
    ctx = (mxq(e, 3, "e4m3") @ mxq(vw, 2, "e4m3")) / e.sum(-1, keepdims=True)
    return ctx.reshape(B, S, S, HP, WP, CV).transpose(0, 5, 1, 3, 2, 4).reshape(B, CV, H, W)

@@ -1,0 +1,355 @@
+from contextlib import ExitStack
+
+import concourse.mybir as mybir
+from concourse.masks import make_identity
+
+F32 = mybir.dt.float32
+BF16 = mybir.dt.bfloat16
+U32 = mybir.dt.uint32
+U8 = mybir.dt.uint8
+FP8X4 = mybir.dt.float8_e4m3fn_x4
+ALU = mybir.AluOpType
+ACT = mybir.ActivationFunctionType
+AXIS_X = mybir.AxisListType.X
+
+P = 128
+PACK = 4
+C_IN = 1024
+C_OUT = 512
+C_QK = 128
+PIXELS = 4096
+HALF_MAP = 2048
+WIN = 32
+TOKENS = 1024
+PASS = 512
+WINDOWS = 4
+TILES = 32
+UNITS = 8
+SCALE = C_QK ** -0.5
+
+FLOPS = 2 * C_OUT * C_IN * PIXELS + WINDOWS * 2 * TOKENS * TOKENS * (C_QK + C_OUT)
+
+
+def tile_pyramidselfattentionblock_pa_t_kernel(tc, x, q, k, v_w, v_b, out):
+    nc = tc.nc
+    x_rows = x.rearrange("b c h w -> (b c) (h w)")
+    q_rows = q.rearrange("b c h w -> (b c) (h w)")
+    k_rows = k.rearrange("b c h w -> (b c) (h w)")
+    out_rows = out.rearrange("b o h w -> (b o) (h w)")
+
+    with ExitStack() as stack:
+        keep = stack.enter_context(tc.tile_pool(name="keep", bufs=1))
+        maps = stack.enter_context(tc.tile_pool(name="maps", bufs=2))
+        xq = stack.enter_context(tc.tile_pool(name="xq", bufs=2))
+        val = stack.enter_context(tc.tile_pool(name="val", bufs=2))
+        att = stack.enter_context(tc.tile_pool(name="att", bufs=3))
+        psum = stack.enter_context(tc.psum_pool(name="psum", bufs=1))
+
+        ident = keep.tile([P, P], F32)
+        make_identity(nc, ident[:])
+        bias_sb = keep.tile([P, C_OUT], BF16)
+        w_codes = keep.tile([P, 2, C_OUT], U32, align_bytes=64)
+        w_scales = keep.tile([P, 2, C_OUT], U8, align_bytes=64)
+
+        q_raw = {}
+        k_raw = {}
+        x_raw = {}
+        q_win = {}
+        k_win = {}
+        x_grouped = {}
+        x_codes = {}
+        x_scales = {}
+        v_grouped = {}
+        v_codes = {}
+        v_scales = {}
+        sim = {}
+        e_rows = {}
+        e_sums = {}
+        e_grouped = {}
+        e_codes = {}
+        e_scales = {}
+        r_cols = {}
+        stage = {}
+
+        def load_qk(a):
+            q_raw[a] = maps.tile([P, HALF_MAP], BF16, name="q_raw%d" % a, tag="q_raw")
+            nc.sync.dma_start(out=q_raw[a][:], in_=q_rows[:, HALF_MAP * a : HALF_MAP * (a + 1)])
+            k_raw[a] = maps.tile([P, HALF_MAP], BF16, name="k_raw%d" % a, tag="k_raw")
+            nc.sync.dma_start(out=k_raw[a][:], in_=k_rows[:, HALF_MAP * a : HALF_MAP * (a + 1)])
+
+        def load_x_chunk(a, tg):
+            chunk = maps.tile([P, 8, 1024], BF16, name="x_raw%d%d" % (a, tg), tag="x_raw", bufs=4)
+            first = HALF_MAP * a + 1024 * tg
+            for gu in range(4):
+                nc.sync.dma_start(
+                    out=chunk[:, 2 * gu : 2 * gu + 2, :],
+                    in_=x_rows[256 * gu : 256 * (gu + 1), first : first + 1024].rearrange(
+                        "(p e) w -> p e w", e=2
+                    ),
+                )
+            x_raw[(a, tg)] = chunk
+
+        def window_maps(w):
+            a, d = w // 2, w % 2
+            engine = nc.vector if w == 0 else nc.gpsimd
+            q_win[w] = maps.tile([P, TOKENS], BF16, name="q_win%d" % w, tag="q_win")
+            engine.tensor_copy(
+                out=q_win[w][:].rearrange("c (i j) -> c i j", j=WIN),
+                in_=q_raw[a][:].rearrange("c (i d j) -> c d i j", d=2, j=WIN)[:, d],
+            )
+            k_win[w] = maps.tile([P, TOKENS], BF16, name="k_win%d" % w, tag="k_win")
+            engine.tensor_copy(
+                out=k_win[w][:].rearrange("c (tu r j e) -> c tu r j e", r=4, j=WIN, e=2),
+                in_=k_raw[a][:].rearrange(
+                    "c (tu e r d j) -> c d tu r j e", e=2, r=4, d=2, j=WIN
+                )[:, d],
+            )
+
+        def scores(i):
+            w, lt8 = i // 8, i % 8
+            lo = psum.tile([P, PASS], F32, name="sim_lo%d" % i, tag="sim_lo", bufs=2)
+            hi = psum.tile([P, PASS], F32, name="sim_hi%d" % i, tag="sim_hi", bufs=2)
+            sim[i] = (lo, hi)
+            for h in range(2):
+                nc.tensor.matmul(
+                    out=sim[i][h][:],
+                    lhsT=q_win[w][:, P * lt8 : P * (lt8 + 1)],
+                    rhs=k_win[w][:, PASS * h : PASS * (h + 1)],
+                    start=True,
+                    stop=True,
+                )
+
+        def soften(i):
+            u, lt = i // 4, i % 4
+            if lt == 0:
+                e_sums[u] = att.tile([P, 4, 2], F32, name="e_sums%d" % u, tag="e_sums")
+            half_max = att.tile([P, 2], F32, name="half_max%d" % i, tag="half_max")
+            for h in range(2):
+                nc.vector.reduce_max(out=half_max[:, h : h + 1], in_=sim[i][h][:], axis=AXIS_X)
+            neg_max = att.tile([P, 1], F32, name="neg_max%d" % i, tag="neg_max")
+            nc.vector.tensor_scalar(
+                out=neg_max[:],
+                in0=half_max[:, 0:1],
+                scalar1=half_max[:, 1:2],
+                scalar2=-SCALE,
+                op0=ALU.max,
+                op1=ALU.mult,
+            )
+            e_rows[i] = att.tile([P, TOKENS], BF16, name="e_rows%d" % i, tag="e_rows")
+            for h in range(2):
+                nc.scalar.activation(
+                    out=e_rows[i][:, PASS * h : PASS * (h + 1)],
+                    in_=sim[i][h][:],
+                    func=ACT.Exp,
+                    bias=neg_max[:, 0:1],
+                    scale=SCALE,
+                    accum_out=e_sums[u][:, lt, h : h + 1],
+                )
+
+        def turn(i):
+            u, lt = i // 4, i % 4
+            if lt == 0:
+                e_grouped[u] = att.tile(
+                    [P, 2, PASS, PACK], BF16, name="e_grouped%d" % u, tag="e_grouped", bufs=2,
+                    align_bytes=64,
+                )
+            turned = psum.tile([P, 4, P], F32, name="turned%d" % i, tag="turn", bufs=2)
+            e_words = e_rows[i][:].bitcast(F32)
+            for tu in range(4):
+                nc.tensor.transpose(turned[:, tu, :], e_words[:, P * tu : P * (tu + 1)], ident[:])
+            nc.scalar.copy(
+                out=e_grouped[u][:].bitcast(F32)[:, :, P * lt : P * (lt + 1), :],
+                in_=turned[:].rearrange("p (g u) l -> p g l u", u=2),
+            )
+
+        def finish_unit(u):
+            row_sum = att.tile([P, 4], F32, name="row_sum%d" % u, tag="row_sum")
+            nc.vector.tensor_reduce(out=row_sum[:], in_=e_sums[u][:], axis=AXIS_X, op=ALU.add)
+            row_inv = att.tile([P, 4], F32, name="row_inv%d" % u, tag="row_inv")
+            nc.vector.reciprocal(out=row_inv[:], in_=row_sum[:])
+            spread = psum.tile([P, PASS], F32, name="spread%d" % u, tag="turn", bufs=2)
+            for lt in range(4):
+                nc.tensor.matmul(
+                    out=spread[:, P * lt : P * (lt + 1)],
+                    lhsT=row_inv[:, lt : lt + 1].to_broadcast([P, P]),
+                    rhs=ident[:],
+                    start=True,
+                    stop=True,
+                )
+            r_cols[u] = att.tile([P, PASS], F32, name="r_cols%d" % u, tag="r_cols")
+            nc.scalar.copy(out=r_cols[u][:], in_=spread[:])
+            e_codes[u] = att.tile([P, 2, PASS], U32, name="e_codes%d" % u, tag="e_codes", align_bytes=64)
+            e_scales[u] = att.tile([P, 2, PASS], U8, name="e_scales%d" % u, tag="e_scales", align_bytes=64)
+            for tg in range(2):
+                nc.vector.quantize_mx(
+                    out=e_codes[u][:, tg, :].bitcast(FP8X4),
+                    scales=e_scales[u][:, tg, :],
+                    in_=e_grouped[u][:, tg].rearrange("p l t -> p (l t)"),
+                )
+
+        def regroup_x(pair, g):
+            w, tg = pair // 2, pair % 2
+            a, d = w // 2, w % 2
+            grouped = xq.tile(
+                [P, PASS, PACK], BF16, name="x_grouped%d%d" % (pair, g), tag="x_grouped", bufs=4,
+                align_bytes=64,
+            )
+            x_grouped[(pair, g)] = grouped
+            planes = x_raw[(a, tg)][:, PACK * g : PACK * (g + 1), :]
+            if w == 0:
+                nc.vector.tensor_copy(
+                    out=grouped[:].rearrange("p (r c i) t -> p r c t i", c=8, i=4),
+                    in_=planes.rearrange("p t (r d c i) -> p d r c t i", d=2, c=8, i=4)[:, d],
+                )
+            else:
+                nc.scalar.copy(
+                    out=grouped[:].rearrange("p (r j) t -> p r j t", j=WIN),
+                    in_=planes.rearrange("p t (r d j) -> p d r j t", d=2, j=WIN)[:, d],
+                )
+
+        def quantise_x(pair, g):
+            w, tg = pair // 2, pair % 2
+            if tg == 0 and g == 0:
+                x_codes[w] = xq.tile([P, 2, TOKENS], U32, name="x_codes%d" % w, tag="x_codes", align_bytes=64)
+                x_scales[w] = xq.tile([P, 2, TOKENS], U8, name="x_scales%d" % w, tag="x_scales", align_bytes=64)
+            cols = slice(PASS * tg, PASS * (tg + 1))
+            nc.vector.quantize_mx(
+                out=x_codes[w][:, g, cols].bitcast(FP8X4),
+                scales=x_scales[w][:, g, cols],
+                in_=x_grouped[(pair, g)][:].rearrange("p n t -> p (n t)"),
+            )
+
+        def value_block(pair, oc):
+            w, tg = pair // 2, pair % 2
+            if oc == 0:
+                v_grouped[pair] = val.tile(
+                    [P, C_OUT * PACK], BF16, name="v_grouped%d" % pair, tag="v_grouped", align_bytes=64
+                )
+            o_cols = slice(P * oc, P * (oc + 1))
+            v_bank = psum.tile([P, PACK, P], F32, name="v_bank%d%d" % (pair, oc), tag="acc", bufs=2)
+            for t in range(PACK):
+                tok = slice(PASS * tg + P * t, PASS * tg + P * (t + 1))
+                for g in range(2):
+                    nc.tensor.matmul_mx(
+                        out=v_bank[:, t, :],
+                        lhsT=x_codes[w][:, g, tok].bitcast(FP8X4),
+                        lhsT_scale=x_scales[w][:, g, tok],
+                        rhs=w_codes[:, g, o_cols].bitcast(FP8X4),
+                        rhs_scale=w_scales[:, g, o_cols],
+                        start=(g == 0),
+                        stop=(g == 1),
+                    )
+            nc.vector.tensor_tensor(
+                out=v_grouped[pair][:, PASS * oc : PASS * (oc + 1)].rearrange("p (o t) -> p o t", t=PACK),
+                in0=v_bank[:].rearrange("p t o -> p o t"),
+                in1=bias_sb[:, o_cols].unsqueeze(2).to_broadcast([P, P, PACK]),
+                op=ALU.add,
+            )
+
+        def quantise_v(pair):
+            w, tg = pair // 2, pair % 2
+            if tg == 0:
+                v_codes[w] = val.tile([P, 2, C_OUT], U32, name="v_codes%d" % w, tag="v_codes", align_bytes=64)
+                v_scales[w] = val.tile([P, 2, C_OUT], U8, name="v_scales%d" % w, tag="v_scales", align_bytes=64)
+            nc.vector.quantize_mx(
+                out=v_codes[w][:, tg, :].bitcast(FP8X4),
+                scales=v_scales[w][:, tg, :],
+                in_=v_grouped[pair][:],
+            )
+
+        def context_group(u, ot):
+            w, lh = u // 2, u % 2
+            a, d = w // 2, w % 2
+            o_cols = slice(P * ot, P * (ot + 1))
+            c_bank = psum.tile([P, PASS], F32, name="c_bank%d%d" % (u, ot), tag="acc", bufs=2)
+            for tg in range(2):
+                nc.tensor.matmul_mx(
+                    out=c_bank[:],
+                    lhsT=v_codes[w][:, tg, o_cols].bitcast(FP8X4),
+                    lhsT_scale=v_scales[w][:, tg, o_cols],
+                    rhs=e_codes[u][:, tg, :].bitcast(FP8X4),
+                    rhs_scale=e_scales[u][:, tg, :],
+                    start=(tg == 0),
+                    stop=(tg == 1),
+                )
+            if d == 0:
+                stage[(a, lh, ot)] = ost.tile(
+                    [P, 1024], F32, name="stage%d%d%d" % (a, lh, ot), tag="stage%d" % ot
+                )
+            rows = stage[(a, lh, ot)]
+            nc.vector.tensor_tensor(
+                out=rows[:].rearrange("p (i d j) -> p d i j", d=2, j=WIN)[:, d],
+                in0=c_bank[:].rearrange("p (i j) -> p i j", j=WIN),
+                in1=r_cols[u][:].rearrange("p (i j) -> p i j", j=WIN),
+                op=ALU.mult,
+            )
+            if d == 1:
+                first = HALF_MAP * a + 1024 * lh
+                nc.sync.dma_start(out=out_rows[o_cols, first : first + 1024], in_=rows[:])
+
+        load_qk(0)
+        load_x_chunk(0, 0)
+        with tc.tile_pool(name="setup", bufs=1) as setup:
+            w_raw = setup.tile([P, 4, C_IN], BF16)
+            nc.sync.dma_start(out=w_raw[:], in_=v_w.rearrange("(t p) c -> p t c", p=P))
+            nc.sync.dma_start(out=bias_sb[:], in_=v_b.partition_broadcast(P))
+            load_x_chunk(0, 1)
+            load_qk(1)
+            load_x_chunk(1, 0)
+            load_x_chunk(1, 1)
+
+            window_maps(0)
+            scores(0)
+
+            w_grouped = setup.tile([P, 2, C_OUT, PACK], BF16, align_bytes=64)
+            w_words = w_raw[:].bitcast(F32)
+            w_grouped_words = w_grouped[:].bitcast(F32)
+            for g in range(2):
+                for half in range(2):
+                    w_bank = psum.tile([P, 2, 256], F32, name="w_bank%d%d" % (g, half), tag="turn", bufs=2)
+                    for u in range(2):
+                        for o2 in range(2):
+                            nc.tensor.transpose(
+                                w_bank[:, u, P * o2 : P * (o2 + 1)],
+                                w_words[:, 2 * half + o2, P * (2 * g + u) : P * (2 * g + u + 1)],
+                                ident[:],
+                            )
+                    nc.scalar.copy(
+                        out=w_grouped_words[:, g, 256 * half : 256 * (half + 1), :],
+                        in_=w_bank[:].rearrange("p u o -> p o u"),
+                    )
+            for g in range(2):
+                nc.vector.quantize_mx(
+                    out=w_codes[:, g, :].bitcast(FP8X4),
+                    scales=w_scales[:, g, :],
+                    in_=w_grouped[:, g].rearrange("p o t -> p (o t)"),
+                )
+
+        ost = stack.enter_context(tc.tile_pool(name="ost", bufs=2))
+
+        regroup_x(0, 0)
+        regroup_x(0, 1)
+        for u in range(-1, UNITS + 1):
+            for lt in range(4):
+                i = 4 * u + lt
+                if 0 <= u < UNITS:
+                    if i + 1 < TILES:
+                        scores(i + 1)
+                    soften(i)
+                if lt == 0 and u + 1 < UNITS:
+                    quantise_x(u + 1, 0)
+                    quantise_x(u + 1, 1)
+                if lt == 0 and 0 <= u < UNITS:
+                    quantise_v(u)
+                if lt == 0 and u >= 1:
+                    finish_unit(u - 1)
+                if u + 1 < UNITS:
+                    value_block(u + 1, lt)
+                if u >= 1:
+                    context_group(u - 1, lt)
+                if 0 <= u < UNITS:
+                    turn(i)
+                if lt >= 2 and u + 2 < UNITS:
+                    regroup_x(u + 2, lt - 2)
+                if lt == 0 and u % 2 == 0 and 0 <= u and u // 2 + 1 < WINDOWS:
+                    window_maps(u // 2 + 1)

@@ -91,7 +91,7 @@ def tile_pyramidselfattentionblock_pa_t_kernel(tc, x, q, k, v_w, v_b, out):
 
         def window_maps(w):
             a, d = w // 2, w % 2
-            engine = nc.vector if w == 0 else nc.gpsimd
+            engine = nc.vector
             q_win[w] = maps.tile([P, TOKENS], BF16, name="q_win%d" % w, tag="q_win")
             engine.tensor_copy(
                 out=q_win[w][:].rearrange("c (i j) -> c i j", j=WIN),

@@ -19,12 +19,20 @@ C_OUT = 512
 C_QK = 128
 PIXELS = 4096
 HALF_MAP = 2048
+CHUNK = 1024
 WIN = 32
 TOKENS = 1024
 PASS = 512
 WINDOWS = 4
 TILES = 32
 UNITS = 8
+PAIRS = 8
+BLOCKS = 32
+GROUPS = 32
+X_STEP = 2
+VALUE_STEP = 6
+CTX_STEP = 14
+WEIGHT_STEP = 3
 SCALE = C_QK ** -0.5
 
 FLOPS = 2 * C_OUT * C_IN * PIXELS + WINDOWS * 2 * TOKENS * TOKENS * (C_QK + C_OUT)
@@ -43,11 +51,14 @@ def tile_pyramidselfattentionblock_pa_t_kernel(tc, x, q, k, v_w, v_b, out):
         xq = stack.enter_context(tc.tile_pool(name="xq", bufs=2))
         val = stack.enter_context(tc.tile_pool(name="val", bufs=2))
         att = stack.enter_context(tc.tile_pool(name="att", bufs=3))
-        psum = stack.enter_context(tc.psum_pool(name="psum", bufs=1))
+        ost = stack.enter_context(tc.tile_pool(name="ost", bufs=2))
+        psum = stack.enter_context(tc.psum_pool(name="psum", bufs=2))
 
         ident = keep.tile([P, P], F32)
         make_identity(nc, ident[:])
         bias_sb = keep.tile([P, C_OUT], BF16)
+        w_raw = keep.tile([P, 4, C_IN], BF16)
+        w_grouped = keep.tile([P, 2, C_OUT, PACK], BF16, align_bytes=64)
         w_codes = keep.tile([P, 2, C_OUT], U32, align_bytes=64)
         w_scales = keep.tile([P, 2, C_OUT], U8, align_bytes=64)
 
@@ -59,16 +70,21 @@ def tile_pyramidselfattentionblock_pa_t_kernel(tc, x, q, k, v_w, v_b, out):
         x_grouped = {}
         x_codes = {}
         x_scales = {}
+        v_bank = {}
         v_grouped = {}
         v_codes = {}
         v_scales = {}
         sim = {}
+        neg_max = {}
         e_rows = {}
+        turned = {}
         e_sums = {}
         e_grouped = {}
         e_codes = {}
         e_scales = {}
+        row_inv = {}
         r_cols = {}
+        c_bank = {}
         stage = {}
 
         def load_qk(a):
@@ -78,37 +94,42 @@ def tile_pyramidselfattentionblock_pa_t_kernel(tc, x, q, k, v_w, v_b, out):
             nc.sync.dma_start(out=k_raw[a][:], in_=k_rows[:, HALF_MAP * a : HALF_MAP * (a + 1)])
 
         def load_x_chunk(a, tg):
-            chunk = maps.tile([P, 8, 1024], BF16, name="x_raw%d%d" % (a, tg), tag="x_raw", bufs=4)
-            first = HALF_MAP * a + 1024 * tg
+            chunk = maps.tile([P, 8, CHUNK], BF16, name="x_raw%d%d" % (a, tg), tag="x_raw", bufs=3)
+            first = HALF_MAP * a + CHUNK * tg
             for gu in range(4):
                 nc.sync.dma_start(
                     out=chunk[:, 2 * gu : 2 * gu + 2, :],
-                    in_=x_rows[256 * gu : 256 * (gu + 1), first : first + 1024].rearrange(
+                    in_=x_rows[256 * gu : 256 * (gu + 1), first : first + CHUNK].rearrange(
                         "(p e) w -> p e w", e=2
                     ),
                 )
             x_raw[(a, tg)] = chunk
 
-        def window_maps(w):
+        def query_map(w, copy):
             a, d = w // 2, w % 2
-            engine = nc.vector
             q_win[w] = maps.tile([P, TOKENS], BF16, name="q_win%d" % w, tag="q_win")
-            engine.tensor_copy(
+            copy(
                 out=q_win[w][:].rearrange("c (i j) -> c i j", j=WIN),
                 in_=q_raw[a][:].rearrange("c (i d j) -> c d i j", d=2, j=WIN)[:, d],
             )
-            k_win[w] = maps.tile([P, TOKENS], BF16, name="k_win%d" % w, tag="k_win")
-            engine.tensor_copy(
-                out=k_win[w][:].rearrange("c (tu r j e) -> c tu r j e", r=4, j=WIN, e=2),
+
+        def key_map_quarter(w, tu, copy):
+            a, d = w // 2, w % 2
+            if tu == 0:
+                k_win[w] = maps.tile([P, TOKENS], BF16, name="k_win%d" % w, tag="k_win")
+            copy(
+                out=k_win[w][:, 256 * tu : 256 * (tu + 1)].rearrange(
+                    "c (r j e) -> c r j e", j=WIN, e=2
+                ),
                 in_=k_raw[a][:].rearrange(
                     "c (tu e r d j) -> c d tu r j e", e=2, r=4, d=2, j=WIN
-                )[:, d],
+                )[:, d, tu],
             )
 
         def scores(i):
             w, lt8 = i // 8, i % 8
-            lo = psum.tile([P, PASS], F32, name="sim_lo%d" % i, tag="sim_lo", bufs=2)
-            hi = psum.tile([P, PASS], F32, name="sim_hi%d" % i, tag="sim_hi", bufs=2)
+            lo = psum.tile([P, PASS], F32, name="sim_lo%d" % i, tag="sim_lo")
+            hi = psum.tile([P, PASS], F32, name="sim_hi%d" % i, tag="sim_hi")
             sim[i] = (lo, hi)
             for h in range(2):
                 nc.tensor.matmul(
@@ -119,119 +140,117 @@ def tile_pyramidselfattentionblock_pa_t_kernel(tc, x, q, k, v_w, v_b, out):
                     stop=True,
                 )
 
-        def soften(i):
-            u, lt = i // 4, i % 4
-            if lt == 0:
-                e_sums[u] = att.tile([P, 4, 2], F32, name="e_sums%d" % u, tag="e_sums")
+        def row_max(i):
             half_max = att.tile([P, 2], F32, name="half_max%d" % i, tag="half_max")
             for h in range(2):
                 nc.vector.reduce_max(out=half_max[:, h : h + 1], in_=sim[i][h][:], axis=AXIS_X)
-            neg_max = att.tile([P, 1], F32, name="neg_max%d" % i, tag="neg_max")
-            nc.vector.tensor_scalar(
-                out=neg_max[:],
-                in0=half_max[:, 0:1],
-                scalar1=half_max[:, 1:2],
-                scalar2=-SCALE,
-                op0=ALU.max,
-                op1=ALU.mult,
-            )
+            top = att.tile([P, 1], F32, name="top%d" % i, tag="top")
+            nc.vector.reduce_max(out=top[:], in_=half_max[:], axis=AXIS_X)
+            neg_max[i] = att.tile([P, 1], F32, name="neg_max%d" % i, tag="neg_max")
+            nc.scalar.mul(out=neg_max[i][:], in_=top[:], mul=-SCALE)
+
+        def exponent(i):
+            u, lt = i // 4, i % 4
+            if lt == 0:
+                e_sums[u] = att.tile([P, 4, 2], F32, name="e_sums%d" % u, tag="e_sums")
             e_rows[i] = att.tile([P, TOKENS], BF16, name="e_rows%d" % i, tag="e_rows")
             for h in range(2):
                 nc.scalar.activation(
                     out=e_rows[i][:, PASS * h : PASS * (h + 1)],
                     in_=sim[i][h][:],
                     func=ACT.Exp,
-                    bias=neg_max[:, 0:1],
+                    bias=neg_max[i][:, 0:1],
                     scale=SCALE,
                     accum_out=e_sums[u][:, lt, h : h + 1],
                 )
 
-        def turn(i):
+        def turn_matmuls(i):
+            turned[i] = psum.tile([P, 4, P], F32, name="turned%d" % i, tag="turn")
+            e_words = e_rows[i][:].bitcast(F32)
+            for tu in range(4):
+                nc.tensor.transpose(turned[i][:, tu, :], e_words[:, P * tu : P * (tu + 1)], ident[:])
+
+        def turn_copy(i):
             u, lt = i // 4, i % 4
             if lt == 0:
                 e_grouped[u] = att.tile(
                     [P, 2, PASS, PACK], BF16, name="e_grouped%d" % u, tag="e_grouped", bufs=2,
                     align_bytes=64,
                 )
-            turned = psum.tile([P, 4, P], F32, name="turned%d" % i, tag="turn", bufs=2)
-            e_words = e_rows[i][:].bitcast(F32)
-            for tu in range(4):
-                nc.tensor.transpose(turned[:, tu, :], e_words[:, P * tu : P * (tu + 1)], ident[:])
             nc.scalar.copy(
                 out=e_grouped[u][:].bitcast(F32)[:, :, P * lt : P * (lt + 1), :],
-                in_=turned[:].rearrange("p (g u) l -> p g l u", u=2),
+                in_=turned[i][:].rearrange("p (g u) l -> p g l u", u=2),
             )
 
-        def finish_unit(u):
+        def invert_sums(u):
             row_sum = att.tile([P, 4], F32, name="row_sum%d" % u, tag="row_sum")
             nc.vector.tensor_reduce(out=row_sum[:], in_=e_sums[u][:], axis=AXIS_X, op=ALU.add)
-            row_inv = att.tile([P, 4], F32, name="row_inv%d" % u, tag="row_inv")
-            nc.vector.reciprocal(out=row_inv[:], in_=row_sum[:])
-            spread = psum.tile([P, PASS], F32, name="spread%d" % u, tag="turn", bufs=2)
-            for lt in range(4):
-                nc.tensor.matmul(
-                    out=spread[:, P * lt : P * (lt + 1)],
-                    lhsT=row_inv[:, lt : lt + 1].to_broadcast([P, P]),
-                    rhs=ident[:],
-                    start=True,
-                    stop=True,
-                )
-            r_cols[u] = att.tile([P, PASS], F32, name="r_cols%d" % u, tag="r_cols")
-            nc.scalar.copy(out=r_cols[u][:], in_=spread[:])
-            e_codes[u] = att.tile([P, 2, PASS], U32, name="e_codes%d" % u, tag="e_codes", align_bytes=64)
-            e_scales[u] = att.tile([P, 2, PASS], U8, name="e_scales%d" % u, tag="e_scales", align_bytes=64)
-            for tg in range(2):
-                nc.vector.quantize_mx(
-                    out=e_codes[u][:, tg, :].bitcast(FP8X4),
-                    scales=e_scales[u][:, tg, :],
-                    in_=e_grouped[u][:, tg].rearrange("p l t -> p (l t)"),
-                )
+            row_inv[u] = att.tile([P, 4], F32, name="row_inv%d" % u, tag="row_inv")
+            nc.vector.reciprocal(out=row_inv[u][:], in_=row_sum[:])
 
-        def regroup_x(pair, g):
+        def spread_inverse(u):
+            spread = psum.tile([P, PASS], F32, name="spread%d" % u, tag="turn")
+            for lt in range(4):
+                nc.tensor.transpose(
+                    spread[:, P * lt : P * (lt + 1)],
+                    row_inv[u][:, lt : lt + 1].to_broadcast([P, P]),
+                    ident[:],
+                )
+            r_cols[u] = att.tile([P, PASS], F32, name="r_cols%d" % u, tag="r_cols", bufs=4)
+            nc.scalar.copy(out=r_cols[u][:], in_=spread[:])
+
+        def quantise_e(u, tg):
+            if tg == 0:
+                e_codes[u] = att.tile([P, 2, PASS], U32, name="e_codes%d" % u, tag="e_codes", align_bytes=64)
+                e_scales[u] = att.tile([P, 2, PASS], U8, name="e_scales%d" % u, tag="e_scales", align_bytes=64)
+            nc.vector.quantize_mx(
+                out=e_codes[u][:, tg, :].bitcast(FP8X4),
+                scales=e_scales[u][:, tg, :],
+                in_=e_grouped[u][:, tg].rearrange("p l t -> p (l t)"),
+            )
+
+        def regroup_x(pair, quarter):
             w, tg = pair // 2, pair % 2
             a, d = w // 2, w % 2
+            g, hh = quarter // 2, quarter % 2
             grouped = xq.tile(
-                [P, PASS, PACK], BF16, name="x_grouped%d%d" % (pair, g), tag="x_grouped", bufs=4,
-                align_bytes=64,
+                [P, 256, PACK], BF16, name="x_grouped%d%d" % (pair, quarter),
+                tag="x_grouped%d" % quarter, bufs=1, align_bytes=64,
             )
-            x_grouped[(pair, g)] = grouped
-            planes = x_raw[(a, tg)][:, PACK * g : PACK * (g + 1), :]
-            if w == 0:
-                nc.vector.tensor_copy(
-                    out=grouped[:].rearrange("p (r c i) t -> p r c t i", c=8, i=4),
-                    in_=planes.rearrange("p t (r d c i) -> p d r c t i", d=2, c=8, i=4)[:, d],
-                )
-            else:
-                nc.scalar.copy(
-                    out=grouped[:].rearrange("p (r j) t -> p r j t", j=WIN),
-                    in_=planes.rearrange("p t (r d j) -> p d r j t", d=2, j=WIN)[:, d],
-                )
+            x_grouped[(pair, quarter)] = grouped
+            planes = x_raw[(a, tg)][:, PACK * g : PACK * (g + 1), PASS * hh : PASS * (hh + 1)]
+            nc.gpsimd.tensor_scalar(
+                out=grouped[:].rearrange("p (r j) t -> p r j t", j=WIN),
+                in0=planes.rearrange("p t (r d j) -> p d r j t", d=2, j=WIN)[:, d],
+                scalar1=1.0,
+                scalar2=0.0,
+                op0=ALU.mult,
+                op1=ALU.add,
+            )
 
-        def quantise_x(pair, g):
+        def quantise_x(pair, quarter):
             w, tg = pair // 2, pair % 2
-            if tg == 0 and g == 0:
+            g, hh = quarter // 2, quarter % 2
+            if tg == 0 and quarter == 0:
                 x_codes[w] = xq.tile([P, 2, TOKENS], U32, name="x_codes%d" % w, tag="x_codes", align_bytes=64)
                 x_scales[w] = xq.tile([P, 2, TOKENS], U8, name="x_scales%d" % w, tag="x_scales", align_bytes=64)
-            cols = slice(PASS * tg, PASS * (tg + 1))
+            cols = slice(PASS * tg + 256 * hh, PASS * tg + 256 * (hh + 1))
             nc.vector.quantize_mx(
                 out=x_codes[w][:, g, cols].bitcast(FP8X4),
                 scales=x_scales[w][:, g, cols],
-                in_=x_grouped[(pair, g)][:].rearrange("p n t -> p (n t)"),
+                in_=x_grouped[(pair, quarter)][:].rearrange("p n t -> p (n t)"),
             )
 
-        def value_block(pair, oc):
+        def value_matmuls(j):
+            pair, oc = j // 4, j % 4
             w, tg = pair // 2, pair % 2
-            if oc == 0:
-                v_grouped[pair] = val.tile(
-                    [P, C_OUT * PACK], BF16, name="v_grouped%d" % pair, tag="v_grouped", align_bytes=64
-                )
             o_cols = slice(P * oc, P * (oc + 1))
-            v_bank = psum.tile([P, PACK, P], F32, name="v_bank%d%d" % (pair, oc), tag="acc", bufs=2)
+            v_bank[j] = psum.tile([P, PACK, P], F32, name="v_bank%d" % j, tag="acc")
             for t in range(PACK):
                 tok = slice(PASS * tg + P * t, PASS * tg + P * (t + 1))
                 for g in range(2):
                     nc.tensor.matmul_mx(
-                        out=v_bank[:, t, :],
+                        out=v_bank[j][:, t, :],
                         lhsT=x_codes[w][:, g, tok].bitcast(FP8X4),
                         lhsT_scale=x_scales[w][:, g, tok],
                         rhs=w_codes[:, g, o_cols].bitcast(FP8X4),
@@ -239,10 +258,17 @@ def tile_pyramidselfattentionblock_pa_t_kernel(tc, x, q, k, v_w, v_b, out):
                         start=(g == 0),
                         stop=(g == 1),
                     )
+
+        def value_out(j):
+            pair, oc = j // 4, j % 4
+            if oc == 0:
+                v_grouped[pair] = val.tile(
+                    [P, C_OUT * PACK], BF16, name="v_grouped%d" % pair, tag="v_grouped", align_bytes=64
+                )
             nc.vector.tensor_tensor(
                 out=v_grouped[pair][:, PASS * oc : PASS * (oc + 1)].rearrange("p (o t) -> p o t", t=PACK),
-                in0=v_bank[:].rearrange("p t o -> p o t"),
-                in1=bias_sb[:, o_cols].unsqueeze(2).to_broadcast([P, P, PACK]),
+                in0=v_bank[j][:].rearrange("p t o -> p o t"),
+                in1=bias_sb[:, P * oc : P * (oc + 1)].unsqueeze(2).to_broadcast([P, P, PACK]),
                 op=ALU.add,
             )
 
@@ -257,14 +283,14 @@ def tile_pyramidselfattentionblock_pa_t_kernel(tc, x, q, k, v_w, v_b, out):
                 in_=v_grouped[pair][:],
             )
 
-        def context_group(u, ot):
-            w, lh = u // 2, u % 2
-            a, d = w // 2, w % 2
+        def context_matmuls(j):
+            u, ot = j // 4, j % 4
+            w = u // 2
             o_cols = slice(P * ot, P * (ot + 1))
-            c_bank = psum.tile([P, PASS], F32, name="c_bank%d%d" % (u, ot), tag="acc", bufs=2)
+            c_bank[j] = psum.tile([P, PASS], F32, name="c_bank%d" % j, tag="acc")
             for tg in range(2):
                 nc.tensor.matmul_mx(
-                    out=c_bank[:],
+                    out=c_bank[j][:],
                     lhsT=v_codes[w][:, tg, o_cols].bitcast(FP8X4),
                     lhsT_scale=v_scales[w][:, tg, o_cols],
                     rhs=e_codes[u][:, tg, :].bitcast(FP8X4),
@@ -272,41 +298,34 @@ def tile_pyramidselfattentionblock_pa_t_kernel(tc, x, q, k, v_w, v_b, out):
                     start=(tg == 0),
                     stop=(tg == 1),
                 )
+
+        def context_out(j):
+            u, ot = j // 4, j % 4
+            w, lh = u // 2, u % 2
+            a, d = w // 2, w % 2
             if d == 0:
                 stage[(a, lh, ot)] = ost.tile(
-                    [P, 1024], F32, name="stage%d%d%d" % (a, lh, ot), tag="stage%d" % ot
+                    [P, CHUNK], F32, name="stage%d%d%d" % (a, lh, ot), tag="stage%d" % ot
                 )
             rows = stage[(a, lh, ot)]
             nc.vector.tensor_tensor(
                 out=rows[:].rearrange("p (i d j) -> p d i j", d=2, j=WIN)[:, d],
-                in0=c_bank[:].rearrange("p (i j) -> p i j", j=WIN),
+                in0=c_bank[j][:].rearrange("p (i j) -> p i j", j=WIN),
                 in1=r_cols[u][:].rearrange("p (i j) -> p i j", j=WIN),
                 op=ALU.mult,
             )
             if d == 1:
-                first = HALF_MAP * a + 1024 * lh
-                nc.sync.dma_start(out=out_rows[o_cols, first : first + 1024], in_=rows[:])
+                first = HALF_MAP * a + CHUNK * lh
+                nc.sync.dma_start(
+                    out=out_rows[P * ot : P * (ot + 1), first : first + CHUNK], in_=rows[:]
+                )
 
-        load_qk(0)
-        load_x_chunk(0, 0)
-        with tc.tile_pool(name="setup", bufs=1) as setup:
-            w_raw = setup.tile([P, 4, C_IN], BF16)
-            nc.sync.dma_start(out=w_raw[:], in_=v_w.rearrange("(t p) c -> p t c", p=P))
-            nc.sync.dma_start(out=bias_sb[:], in_=v_b.partition_broadcast(P))
-            load_x_chunk(0, 1)
-            load_qk(1)
-            load_x_chunk(1, 0)
-            load_x_chunk(1, 1)
-
-            window_maps(0)
-            scores(0)
-
-            w_grouped = setup.tile([P, 2, C_OUT, PACK], BF16, align_bytes=64)
+        def transpose_weights():
             w_words = w_raw[:].bitcast(F32)
             w_grouped_words = w_grouped[:].bitcast(F32)
             for g in range(2):
                 for half in range(2):
-                    w_bank = psum.tile([P, 2, 256], F32, name="w_bank%d%d" % (g, half), tag="turn", bufs=2)
+                    w_bank = psum.tile([P, 2, 256], F32, name="w_bank%d%d" % (g, half), tag="turn")
                     for u in range(2):
                         for o2 in range(2):
                             nc.tensor.transpose(
@@ -318,6 +337,8 @@ def tile_pyramidselfattentionblock_pa_t_kernel(tc, x, q, k, v_w, v_b, out):
                         out=w_grouped_words[:, g, 256 * half : 256 * (half + 1), :],
                         in_=w_bank[:].rearrange("p u o -> p o u"),
                     )
+
+        def quantise_weights():
             for g in range(2):
                 nc.vector.quantize_mx(
                     out=w_codes[:, g, :].bitcast(FP8X4),
@@ -325,31 +346,61 @@ def tile_pyramidselfattentionblock_pa_t_kernel(tc, x, q, k, v_w, v_b, out):
                     in_=w_grouped[:, g].rearrange("p o t -> p (o t)"),
                 )
 
-        ost = stack.enter_context(tc.tile_pool(name="ost", bufs=2))
+        load_qk(0)
+        load_x_chunk(0, 0)
+        nc.sync.dma_start(out=w_raw[:], in_=v_w.rearrange("(t p) c -> p t c", p=P))
+        nc.sync.dma_start(out=bias_sb[:], in_=v_b.partition_broadcast(P))
+        load_x_chunk(0, 1)
+        load_qk(1)
+        load_x_chunk(1, 0)
+        load_x_chunk(1, 1)
 
-        regroup_x(0, 0)
-        regroup_x(0, 1)
-        for u in range(-1, UNITS + 1):
-            for lt in range(4):
-                i = 4 * u + lt
-                if 0 <= u < UNITS:
-                    if i + 1 < TILES:
-                        scores(i + 1)
-                    soften(i)
-                if lt == 0 and u + 1 < UNITS:
-                    quantise_x(u + 1, 0)
-                    quantise_x(u + 1, 1)
-                if lt == 0 and 0 <= u < UNITS:
-                    quantise_v(u)
-                if lt == 0 and u >= 1:
-                    finish_unit(u - 1)
-                if u + 1 < UNITS:
-                    value_block(u + 1, lt)
-                if u >= 1:
-                    context_group(u - 1, lt)
-                if 0 <= u < UNITS:
-                    turn(i)
-                if lt >= 2 and u + 2 < UNITS:
-                    regroup_x(u + 2, lt - 2)
-                if lt == 0 and u % 2 == 0 and 0 <= u and u // 2 + 1 < WINDOWS:
-                    window_maps(u // 2 + 1)
+        query_map(0, nc.vector.tensor_copy)
+        for tu in range(4):
+            key_map_quarter(0, tu, nc.vector.tensor_copy)
+        scores(0)
+        for quarter in range(4):
+            regroup_x(0, quarter)
+
+        for s in range(TILES + CTX_STEP):
+            block = s - VALUE_STEP
+            group = s - CTX_STEP
+            if 0 <= block < BLOCKS:
+                value_matmuls(block)
+            if 0 <= group < GROUPS:
+                context_matmuls(group)
+            if 1 <= s <= TILES:
+                turn_matmuls(s - 1)
+            if s + 1 < TILES:
+                scores(s + 1)
+            if s < TILES:
+                row_max(s)
+                exponent(s)
+            if s == WEIGHT_STEP:
+                transpose_weights()
+            if 1 <= s <= TILES:
+                turn_copy(s - 1)
+            if 0 <= block < BLOCKS:
+                value_out(block)
+            if 0 <= group < GROUPS:
+                context_out(group)
+            next_w = s // 8 + 1
+            if next_w < WINDOWS and s % 8 < 4:
+                key_map_quarter(next_w, s % 8, nc.scalar.copy)
+            if next_w < WINDOWS and s % 8 == 4:
+                query_map(next_w, nc.scalar.copy)
+            if s % 4 == 0 and 1 <= s // 4 <= UNITS:
+                invert_sums(s // 4 - 1)
+            if s % 4 == 1 and 1 <= s // 4 <= UNITS:
+                spread_inverse(s // 4 - 1)
+            if s % 4 >= 2 and 1 <= s // 4 <= UNITS:
+                quantise_e(s // 4 - 1, s % 4 - 2)
+            if s == WEIGHT_STEP + 1:
+                quantise_weights()
+            if block % 4 == 3 and 0 <= block < BLOCKS:
+                quantise_v(block // 4)
+            x_quarter = s - X_STEP
+            if 0 <= x_quarter < 4 * PAIRS:
+                quantise_x(x_quarter // 4, x_quarter % 4)
+                if x_quarter // 4 + 1 < PAIRS:
+                    regroup_x(x_quarter // 4 + 1, x_quarter % 4)

@@ -56,7 +56,8 @@ def tile_pyramidselfattentionblock_pa_t_kernel(tc, x, q, k, v_w, v_b, out):
 
         ident = keep.tile([P, P], F32)
         make_identity(nc, ident[:])
-        bias_sb = keep.tile([P, C_OUT], BF16)
+        bias_bf = keep.tile([P, 4], BF16)
+        bias_col = keep.tile([P, 4], F32)
         w_raw = keep.tile([P, 4, C_IN], BF16)
         w_grouped = keep.tile([P, 2, C_OUT, PACK], BF16, align_bytes=64)
         w_codes = keep.tile([P, 2, C_OUT], U32, align_bytes=64)
@@ -66,11 +67,11 @@ def tile_pyramidselfattentionblock_pa_t_kernel(tc, x, q, k, v_w, v_b, out):
         k_raw = {}
         x_raw = {}
         q_win = {}
-        k_win = {}
         x_grouped = {}
         x_codes = {}
         x_scales = {}
         v_bank = {}
+        v_rows = {}
         v_grouped = {}
         v_codes = {}
         v_scales = {}
@@ -105,37 +106,26 @@ def tile_pyramidselfattentionblock_pa_t_kernel(tc, x, q, k, v_w, v_b, out):
                 )
             x_raw[(a, tg)] = chunk
 
-        def query_map(w, copy):
+        def query_map(w):
             a, d = w // 2, w % 2
             q_win[w] = maps.tile([P, TOKENS], BF16, name="q_win%d" % w, tag="q_win")
-            copy(
+            nc.vector.tensor_copy(
                 out=q_win[w][:].rearrange("c (i j) -> c i j", j=WIN),
                 in_=q_raw[a][:].rearrange("c (i d j) -> c d i j", d=2, j=WIN)[:, d],
             )
 
-        def key_map_quarter(w, tu, copy):
-            a, d = w // 2, w % 2
-            if tu == 0:
-                k_win[w] = maps.tile([P, TOKENS], BF16, name="k_win%d" % w, tag="k_win")
-            copy(
-                out=k_win[w][:, 256 * tu : 256 * (tu + 1)].rearrange(
-                    "c (r j e) -> c r j e", j=WIN, e=2
-                ),
-                in_=k_raw[a][:].rearrange(
-                    "c (tu e r d j) -> c d tu r j e", e=2, r=4, d=2, j=WIN
-                )[:, d, tu],
-            )
-
         def scores(i):
             w, lt8 = i // 8, i % 8
+            a, d = w // 2, w % 2
+            keys = k_raw[a][:].rearrange("c (h i d j) -> c d h i j", h=2, d=2, j=WIN)
             lo = psum.tile([P, PASS], F32, name="sim_lo%d" % i, tag="sim_lo")
             hi = psum.tile([P, PASS], F32, name="sim_hi%d" % i, tag="sim_hi")
             sim[i] = (lo, hi)
             for h in range(2):
                 nc.tensor.matmul(
-                    out=sim[i][h][:],
+                    out=sim[i][h][:].rearrange("p (i j) -> p i j", j=WIN),
                     lhsT=q_win[w][:, P * lt8 : P * (lt8 + 1)],
-                    rhs=k_win[w][:, PASS * h : PASS * (h + 1)],
+                    rhs=keys[:, d, h],
                     start=True,
                     stop=True,
                 )
@@ -144,10 +134,15 @@ def tile_pyramidselfattentionblock_pa_t_kernel(tc, x, q, k, v_w, v_b, out):
             half_max = att.tile([P, 2], F32, name="half_max%d" % i, tag="half_max")
             for h in range(2):
                 nc.vector.reduce_max(out=half_max[:, h : h + 1], in_=sim[i][h][:], axis=AXIS_X)
-            top = att.tile([P, 1], F32, name="top%d" % i, tag="top")
-            nc.vector.reduce_max(out=top[:], in_=half_max[:], axis=AXIS_X)
             neg_max[i] = att.tile([P, 1], F32, name="neg_max%d" % i, tag="neg_max")
-            nc.scalar.mul(out=neg_max[i][:], in_=top[:], mul=-SCALE)
+            nc.vector.tensor_scalar(
+                out=neg_max[i][:],
+                in0=half_max[:, 0:1],
+                scalar1=half_max[:, 1:2],
+                scalar2=-SCALE,
+                op0=ALU.max,
+                op1=ALU.mult,
+            )
 
         def exponent(i):
             u, lt = i // 4, i % 4
@@ -242,34 +237,48 @@ def tile_pyramidselfattentionblock_pa_t_kernel(tc, x, q, k, v_w, v_b, out):
             )
 
         def value_matmuls(j):
-            pair, oc = j // 4, j % 4
+            pair, ot = j // 4, j % 4
             w, tg = pair // 2, pair % 2
-            o_cols = slice(P * oc, P * (oc + 1))
-            v_bank[j] = psum.tile([P, PACK, P], F32, name="v_bank%d" % j, tag="acc")
-            for t in range(PACK):
-                tok = slice(PASS * tg + P * t, PASS * tg + P * (t + 1))
-                for g in range(2):
-                    nc.tensor.matmul_mx(
-                        out=v_bank[j][:, t, :],
-                        lhsT=x_codes[w][:, g, tok].bitcast(FP8X4),
-                        lhsT_scale=x_scales[w][:, g, tok],
-                        rhs=w_codes[:, g, o_cols].bitcast(FP8X4),
-                        rhs_scale=w_scales[:, g, o_cols],
-                        start=(g == 0),
-                        stop=(g == 1),
-                    )
+            o_cols = slice(P * ot, P * (ot + 1))
+            tok = slice(PASS * tg, PASS * (tg + 1))
+            v_bank[j] = psum.tile([P, PASS], F32, name="v_bank%d" % j, tag="acc")
+            for g in range(2):
+                nc.tensor.matmul_mx(
+                    out=v_bank[j][:],
+                    lhsT=w_codes[:, g, o_cols].bitcast(FP8X4),
+                    lhsT_scale=w_scales[:, g, o_cols],
+                    rhs=x_codes[w][:, g, tok].bitcast(FP8X4),
+                    rhs_scale=x_scales[w][:, g, tok],
+                    start=(g == 0),
+                    stop=(g == 1),
+                )
 
         def value_out(j):
-            pair, oc = j // 4, j % 4
-            if oc == 0:
+            ot = j % 4
+            v_rows[j] = val.tile([P, PASS], BF16, name="v_rows%d" % j, tag="v_rows", bufs=4)
+            nc.scalar.activation(
+                out=v_rows[j][:],
+                in_=v_bank[j][:],
+                func=ACT.Identity,
+                bias=bias_col[:, ot : ot + 1],
+                scale=1.0,
+            )
+
+        def value_turn(pair, half):
+            if half == 0:
                 v_grouped[pair] = val.tile(
-                    [P, C_OUT * PACK], BF16, name="v_grouped%d" % pair, tag="v_grouped", align_bytes=64
+                    [P, C_OUT, PACK], BF16, name="v_grouped%d" % pair, tag="v_grouped", align_bytes=64
                 )
-            nc.vector.tensor_tensor(
-                out=v_grouped[pair][:, PASS * oc : PASS * (oc + 1)].rearrange("p (o t) -> p o t", t=PACK),
-                in0=v_bank[j][:].rearrange("p t o -> p o t"),
-                in1=bias_sb[:, P * oc : P * (oc + 1)].unsqueeze(2).to_broadcast([P, P, PACK]),
-                op=ALU.add,
+            vt_bank = psum.tile([P, 2, 256], F32, name="vt_bank%d%d" % (pair, half), tag="turn")
+            for o2 in range(2):
+                v_words = v_rows[4 * pair + 2 * half + o2][:].bitcast(F32)
+                for u in range(2):
+                    nc.tensor.transpose(
+                        vt_bank[:, u, P * o2 : P * (o2 + 1)], v_words[:, P * u : P * (u + 1)], ident[:]
+                    )
+            nc.vector.tensor_copy(
+                out=v_grouped[pair][:].bitcast(F32)[:, 256 * half : 256 * (half + 1), :],
+                in_=vt_bank[:].rearrange("p u o -> p o u"),
             )
 
         def quantise_v(pair):
@@ -280,7 +289,7 @@ def tile_pyramidselfattentionblock_pa_t_kernel(tc, x, q, k, v_w, v_b, out):
             nc.vector.quantize_mx(
                 out=v_codes[w][:, tg, :].bitcast(FP8X4),
                 scales=v_scales[w][:, tg, :],
-                in_=v_grouped[pair][:],
+                in_=v_grouped[pair][:].rearrange("p o t -> p (o t)"),
             )
 
         def context_matmuls(j):
@@ -349,16 +358,16 @@ def tile_pyramidselfattentionblock_pa_t_kernel(tc, x, q, k, v_w, v_b, out):
         load_qk(0)
         load_x_chunk(0, 0)
         nc.sync.dma_start(out=w_raw[:], in_=v_w.rearrange("(t p) c -> p t c", p=P))
-        nc.sync.dma_start(out=bias_sb[:], in_=v_b.partition_broadcast(P))
+        with nc.allow_non_contiguous_dma(reason="512 bias values, one to a partition and column"):
+            nc.sync.dma_start(out=bias_bf[:], in_=v_b.rearrange("(t p) -> p t", p=P))
         load_x_chunk(0, 1)
         load_qk(1)
         load_x_chunk(1, 0)
         load_x_chunk(1, 1)
 
-        query_map(0, nc.vector.tensor_copy)
-        for tu in range(4):
-            key_map_quarter(0, tu, nc.vector.tensor_copy)
+        query_map(0)
         scores(0)
+        nc.vector.tensor_copy(out=bias_col[:], in_=bias_bf[:])
         for quarter in range(4):
             regroup_x(0, quarter)
 
@@ -382,13 +391,12 @@ def tile_pyramidselfattentionblock_pa_t_kernel(tc, x, q, k, v_w, v_b, out):
                 turn_copy(s - 1)
             if 0 <= block < BLOCKS:
                 value_out(block)
+                if block % 2 == 1:
+                    value_turn(block // 4, block % 4 // 2)
             if 0 <= group < GROUPS:
                 context_out(group)
-            next_w = s // 8 + 1
-            if next_w < WINDOWS and s % 8 < 4:
-                key_map_quarter(next_w, s % 8, nc.scalar.copy)
-            if next_w < WINDOWS and s % 8 == 4:
-                query_map(next_w, nc.scalar.copy)
+            if s % 8 == 4 and s // 8 + 1 < WINDOWS:
+                query_map(s // 8 + 1)
             if s % 4 == 0 and 1 <= s // 4 <= UNITS:
                 invert_sums(s // 4 - 1)
             if s % 4 == 1 and 1 <= s // 4 <= UNITS:

@@ -29,10 +29,10 @@ UNITS = 8
 PAIRS = 8
 BLOCKS = 32
 GROUPS = 32
-X_STEP = 2
-VALUE_STEP = 6
-CTX_STEP = 14
-WEIGHT_STEP = 3
+X_STEP = 0
+VALUE_STEP = 4
+CTX_STEP = 12
+WEIGHT_STEP = 1
 SCALE = C_QK ** -0.5
 
 FLOPS = 2 * C_OUT * C_IN * PIXELS + WINDOWS * 2 * TOKENS * TOKENS * (C_QK + C_OUT)
@@ -56,8 +56,7 @@ def tile_pyramidselfattentionblock_pa_t_kernel(tc, x, q, k, v_w, v_b, out):
 
         ident = keep.tile([P, P], F32)
         make_identity(nc, ident[:])
-        bias_bf = keep.tile([P, 4], BF16)
-        bias_col = keep.tile([P, 4], F32)
+        bias_sb = keep.tile([P, C_OUT], BF16)
         w_raw = keep.tile([P, 4, C_IN], BF16)
         w_grouped = keep.tile([P, 2, C_OUT, PACK], BF16, align_bytes=64)
         w_codes = keep.tile([P, 2, C_OUT], U32, align_bytes=64)
@@ -71,7 +70,6 @@ def tile_pyramidselfattentionblock_pa_t_kernel(tc, x, q, k, v_w, v_b, out):
         x_codes = {}
         x_scales = {}
         v_bank = {}
-        v_rows = {}
         v_grouped = {}
         v_codes = {}
         v_scales = {}
@@ -207,21 +205,22 @@ def tile_pyramidselfattentionblock_pa_t_kernel(tc, x, q, k, v_w, v_b, out):
         def regroup_x(pair, quarter):
             w, tg = pair // 2, pair % 2
             a, d = w // 2, w % 2
-            g, hh = quarter // 2, quarter % 2
+            g, u = quarter // 2, quarter % 2
             grouped = xq.tile(
                 [P, 256, PACK], BF16, name="x_grouped%d%d" % (pair, quarter),
                 tag="x_grouped%d" % quarter, bufs=1, align_bytes=64,
             )
             x_grouped[(pair, quarter)] = grouped
-            planes = x_raw[(a, tg)][:, PACK * g : PACK * (g + 1), PASS * hh : PASS * (hh + 1)]
-            nc.gpsimd.tensor_scalar(
-                out=grouped[:].rearrange("p (r j) t -> p r j t", j=WIN),
-                in0=planes.rearrange("p t (r d j) -> p d r j t", d=2, j=WIN)[:, d],
-                scalar1=1.0,
-                scalar2=0.0,
-                op0=ALU.mult,
-                op1=ALU.add,
-            )
+            planes = x_raw[(a, tg)][:, PACK * g : PACK * (g + 1), PASS * u : PASS * (u + 1)]
+            for e in range(2):
+                nc.gpsimd.tensor_scalar(
+                    out=grouped[:, P * e : P * (e + 1), :].rearrange("p (r jj) t -> p r jj t", jj=16),
+                    in0=planes.rearrange("p t (r d jj e) -> p d e r jj t", d=2, jj=16, e=2)[:, d, e],
+                    scalar1=1.0,
+                    scalar2=0.0,
+                    op0=ALU.mult,
+                    op1=ALU.add,
+                )
 
         def quantise_x(pair, quarter):
             w, tg = pair // 2, pair % 2
@@ -237,48 +236,34 @@ def tile_pyramidselfattentionblock_pa_t_kernel(tc, x, q, k, v_w, v_b, out):
             )
 
         def value_matmuls(j):
-            pair, ot = j // 4, j % 4
+            pair, oc = j // 4, j % 4
             w, tg = pair // 2, pair % 2
-            o_cols = slice(P * ot, P * (ot + 1))
-            tok = slice(PASS * tg, PASS * (tg + 1))
-            v_bank[j] = psum.tile([P, PASS], F32, name="v_bank%d" % j, tag="acc")
-            for g in range(2):
-                nc.tensor.matmul_mx(
-                    out=v_bank[j][:],
-                    lhsT=w_codes[:, g, o_cols].bitcast(FP8X4),
-                    lhsT_scale=w_scales[:, g, o_cols],
-                    rhs=x_codes[w][:, g, tok].bitcast(FP8X4),
-                    rhs_scale=x_scales[w][:, g, tok],
-                    start=(g == 0),
-                    stop=(g == 1),
-                )
+            o_cols = slice(P * oc, P * (oc + 1))
+            v_bank[j] = psum.tile([P, PACK, P], F32, name="v_bank%d" % j, tag="acc")
+            for t in range(PACK):
+                tok = slice(PASS * tg + P * t, PASS * tg + P * (t + 1))
+                for g in range(2):
+                    nc.tensor.matmul_mx(
+                        out=v_bank[j][:, t, :],
+                        lhsT=x_codes[w][:, g, tok].bitcast(FP8X4),
+                        lhsT_scale=x_scales[w][:, g, tok],
+                        rhs=w_codes[:, g, o_cols].bitcast(FP8X4),
+                        rhs_scale=w_scales[:, g, o_cols],
+                        start=(g == 0),
+                        stop=(g == 1),
+                    )
 
         def value_out(j):
-            ot = j % 4
-            v_rows[j] = val.tile([P, PASS], BF16, name="v_rows%d" % j, tag="v_rows", bufs=4)
-            nc.scalar.activation(
-                out=v_rows[j][:],
-                in_=v_bank[j][:],
-                func=ACT.Identity,
-                bias=bias_col[:, ot : ot + 1],
-                scale=1.0,
-            )
-
-        def value_turn(pair, half):
-            if half == 0:
+            pair, oc = j // 4, j % 4
+            if oc == 0:
                 v_grouped[pair] = val.tile(
-                    [P, C_OUT, PACK], BF16, name="v_grouped%d" % pair, tag="v_grouped", align_bytes=64
+                    [P, C_OUT * PACK], BF16, name="v_grouped%d" % pair, tag="v_grouped", align_bytes=64
                 )
-            vt_bank = psum.tile([P, 2, 256], F32, name="vt_bank%d%d" % (pair, half), tag="turn")
-            for o2 in range(2):
-                v_words = v_rows[4 * pair + 2 * half + o2][:].bitcast(F32)
-                for u in range(2):
-                    nc.tensor.transpose(
-                        vt_bank[:, u, P * o2 : P * (o2 + 1)], v_words[:, P * u : P * (u + 1)], ident[:]
-                    )
-            nc.vector.tensor_copy(
-                out=v_grouped[pair][:].bitcast(F32)[:, 256 * half : 256 * (half + 1), :],
-                in_=vt_bank[:].rearrange("p u o -> p o u"),
+            nc.vector.tensor_tensor(
+                out=v_grouped[pair][:, PASS * oc : PASS * (oc + 1)].rearrange("p (o t) -> p o t", t=PACK),
+                in0=v_bank[j][:].rearrange("p t o -> p o t"),
+                in1=bias_sb[:, P * oc : P * (oc + 1)].unsqueeze(2).to_broadcast([P, P, PACK]),
+                op=ALU.add,
             )
 
         def quantise_v(pair):
@@ -289,7 +274,7 @@ def tile_pyramidselfattentionblock_pa_t_kernel(tc, x, q, k, v_w, v_b, out):
             nc.vector.quantize_mx(
                 out=v_codes[w][:, tg, :].bitcast(FP8X4),
                 scales=v_scales[w][:, tg, :],
-                in_=v_grouped[pair][:].rearrange("p o t -> p (o t)"),
+                in_=v_grouped[pair][:],
             )
 
         def context_matmuls(j):
@@ -358,8 +343,7 @@ def tile_pyramidselfattentionblock_pa_t_kernel(tc, x, q, k, v_w, v_b, out):
         load_qk(0)
         load_x_chunk(0, 0)
         nc.sync.dma_start(out=w_raw[:], in_=v_w.rearrange("(t p) c -> p t c", p=P))
-        with nc.allow_non_contiguous_dma(reason="512 bias values, one to a partition and column"):
-            nc.sync.dma_start(out=bias_bf[:], in_=v_b.rearrange("(t p) -> p t", p=P))
+        nc.sync.dma_start(out=bias_sb[:], in_=v_b.partition_broadcast(P))
         load_x_chunk(0, 1)
         load_qk(1)
         load_x_chunk(1, 0)
@@ -367,7 +351,6 @@ def tile_pyramidselfattentionblock_pa_t_kernel(tc, x, q, k, v_w, v_b, out):
 
         query_map(0)
         scores(0)
-        nc.vector.tensor_copy(out=bias_col[:], in_=bias_bf[:])
         for quarter in range(4):
             regroup_x(0, quarter)
 
@@ -391,8 +374,6 @@ def tile_pyramidselfattentionblock_pa_t_kernel(tc, x, q, k, v_w, v_b, out):
                 turn_copy(s - 1)
             if 0 <= block < BLOCKS:
                 value_out(block)
-                if block % 2 == 1:
-                    value_turn(block // 4, block % 4 // 2)
             if 0 <= group < GROUPS:
                 context_out(group)
             if s % 8 == 4 and s // 8 + 1 < WINDOWS:

@@ -20,20 +20,28 @@ C_QK = 128
 PIXELS = 4096
 HALF_MAP = 2048
 CHUNK = 1024
+SLAB = 512
 WIN = 32
 TOKENS = 1024
 PASS = 512
 WINDOWS = 4
 TILES = 32
-UNITS = 8
+UNIT = 256
+UNITS = 16
 PAIRS = 8
 BLOCKS = 32
 GROUPS = 32
-X_STEP = 0
-VALUE_STEP = 4
-CTX_STEP = 12
-WEIGHT_STEP = 1
 SCALE = C_QK ** -0.5
+EB = 8
+XB = 1
+GP = 4
+S0 = 8
+N0 = 9
+FLUSH = 23
+WSC = ((0, 0), (0, 1), (1, 0), (1, 1))
+VS = [-1 if j < 8 else j for j in range(BLOCKS)]
+CS = [c + 9 for c in range(GROUPS)]
+XS = [-1 if n < 12 else n - 4 for n in range(4 * PAIRS)]
 
 FLOPS = 2 * C_OUT * C_IN * PIXELS + WINDOWS * 2 * TOKENS * TOKENS * (C_QK + C_OUT)
 
@@ -51,66 +59,64 @@ def tile_pyramidselfattentionblock_pa_t_kernel(tc, x, q, k, v_w, v_b, out):
         xq = stack.enter_context(tc.tile_pool(name="xq", bufs=2))
         val = stack.enter_context(tc.tile_pool(name="val", bufs=2))
         att = stack.enter_context(tc.tile_pool(name="att", bufs=3))
-        ost = stack.enter_context(tc.tile_pool(name="ost", bufs=2))
+        ost = stack.enter_context(tc.tile_pool(name="ost", bufs=8))
         psum = stack.enter_context(tc.psum_pool(name="psum", bufs=2))
 
-        ident = keep.tile([P, P], F32)
+        ident = keep.tile([P, P], F32, name="ident")
         make_identity(nc, ident[:])
-        bias_sb = keep.tile([P, C_OUT], BF16)
-        w_raw = keep.tile([P, 4, C_IN], BF16)
-        w_grouped = keep.tile([P, 2, C_OUT, PACK], BF16, align_bytes=64)
-        w_codes = keep.tile([P, 2, C_OUT], U32, align_bytes=64)
-        w_scales = keep.tile([P, 2, C_OUT], U8, align_bytes=64)
+        bias_row = keep.tile([P, C_OUT], BF16, name="bias_row")
+        bias_rows = keep.tile([P, C_OUT], F32, name="bias_rows")
+        ones = keep.tile([P, P], BF16, name="ones")
+        warm = keep.tile([P, 1], F32, name="warm")
+        w_codes = keep.tile([P, 2, C_OUT], U32, name="w_codes", align_bytes=64)
+        w_scales = keep.tile([P, 2, C_OUT], U8, name="w_scales", align_bytes=64)
 
-        q_raw = {}
-        k_raw = {}
-        x_raw = {}
-        q_win = {}
-        x_grouped = {}
-        x_codes = {}
-        x_scales = {}
-        v_bank = {}
-        v_grouped = {}
-        v_codes = {}
-        v_scales = {}
-        sim = {}
-        neg_max = {}
-        e_rows = {}
-        turned = {}
-        e_sums = {}
-        e_grouped = {}
-        e_codes = {}
-        e_scales = {}
-        row_inv = {}
-        r_cols = {}
-        c_bank = {}
-        stage = {}
+        q_raw, k_raw, x_raw, q_win = {}, {}, {}, {}
+        x_grouped, x_codes, x_scales = {}, {}, {}
+        v_bank, v_chan, v_turned, v_grouped, v_codes, v_scales = {}, {}, {}, {}, {}, {}
+        sim, half_max, neg_max, e_rows, turned, e_sums = {}, {}, {}, {}, {}, {}
+        e_grouped, e_codes, e_scales, row_inv, r_cols = {}, {}, {}, {}, {}
+        c_bank, stage, spread, row_sum = {}, {}, {}, {}
+        w_raw, w_grouped, w_bank = {}, {}, {}
+        for half in range(2):
+            w_raw[half] = ost.tile([P, 2, C_IN], BF16, name="w_raw%d" % half, tag="stage", align_bytes=64)
+        for g in range(2):
+            w_grouped[g] = ost.tile([P, C_OUT, PACK], BF16, name="w_grouped%d" % g, tag="stage", align_bytes=64)
 
-        def load_qk(a):
+        def alloc_qk(a):
             q_raw[a] = maps.tile([P, HALF_MAP], BF16, name="q_raw%d" % a, tag="q_raw")
-            nc.sync.dma_start(out=q_raw[a][:], in_=q_rows[:, HALF_MAP * a : HALF_MAP * (a + 1)])
             k_raw[a] = maps.tile([P, HALF_MAP], BF16, name="k_raw%d" % a, tag="k_raw")
-            nc.sync.dma_start(out=k_raw[a][:], in_=k_rows[:, HALF_MAP * a : HALF_MAP * (a + 1)])
 
-        def load_x_chunk(a, tg):
-            chunk = maps.tile([P, 8, CHUNK], BF16, name="x_raw%d%d" % (a, tg), tag="x_raw", bufs=3)
-            first = HALF_MAP * a + CHUNK * tg
-            for gu in range(4):
-                nc.sync.dma_start(
-                    out=chunk[:, 2 * gu : 2 * gu + 2, :],
-                    in_=x_rows[256 * gu : 256 * (gu + 1), first : first + CHUNK].rearrange(
-                        "(p e) w -> p e w", e=2
-                    ),
-                )
-            x_raw[(a, tg)] = chunk
+        def load_map(dst, rows, a, lo, hi):
+            nc.sync.dma_start(out=dst[:, lo:hi], in_=rows[:, HALF_MAP * a + lo : HALF_MAP * a + hi])
 
-        def query_map(w):
-            a, d = w // 2, w % 2
-            q_win[w] = maps.tile([P, TOKENS], BF16, name="q_win%d" % w, tag="q_win")
-            nc.vector.tensor_copy(
-                out=q_win[w][:].rearrange("c (i j) -> c i j", j=WIN),
-                in_=q_raw[a][:].rearrange("c (i d j) -> c d i j", d=2, j=WIN)[:, d],
+        def alloc_x(a, tg):
+            x_raw[(a, tg)] = maps.tile(
+                [P, 8, CHUNK], BF16, name="x_raw%d%d" % (a, tg), tag="x_raw", bufs=4
             )
+
+        def load_x(a, tg, gu):
+            first = HALF_MAP * a + CHUNK * tg
+            nc.sync.dma_start(
+                out=x_raw[(a, tg)][:, 2 * gu : 2 * gu + 2, :],
+                in_=x_rows[256 * gu : 256 * (gu + 1), first : first + CHUNK].rearrange(
+                    "(p e) w -> p e w", e=2
+                ),
+            )
+
+        def query_map(w, part, parts, engine="vector"):
+            a, d = w // 2, w % 2
+            if part == 0:
+                q_win[w] = maps.tile([P, TOKENS], BF16, name="q_win%d" % w, tag="q_win")
+            n = TOKENS // parts
+            dst = q_win[w][:, n * part : n * (part + 1)].rearrange("c (i j) -> c i j", j=WIN)
+            src = q_raw[a][:, 2 * n * part : 2 * n * (part + 1)].rearrange(
+                "c (i d j) -> c d i j", d=2, j=WIN
+            )[:, d]
+            if engine == "scalar":
+                nc.scalar.copy(out=dst, in_=src)
+            else:
+                nc.vector.tensor_copy(out=dst, in_=src)
 
         def scores(i):
             w, lt8 = i // 8, i % 8
@@ -128,25 +134,27 @@ def tile_pyramidselfattentionblock_pa_t_kernel(tc, x, q, k, v_w, v_b, out):
                     stop=True,
                 )
 
-        def row_max(i):
-            half_max = att.tile([P, 2], F32, name="half_max%d" % i, tag="half_max")
+        def half_maxima(i):
+            half_max[i] = att.tile([P, 2], F32, name="half_max%d" % i, tag="half_max")
             for h in range(2):
-                nc.vector.reduce_max(out=half_max[:, h : h + 1], in_=sim[i][h][:], axis=AXIS_X)
+                nc.vector.reduce_max(out=half_max[i][:, h : h + 1], in_=sim[i][h][:], axis=AXIS_X)
+
+        def row_max(i):
             neg_max[i] = att.tile([P, 1], F32, name="neg_max%d" % i, tag="neg_max")
             nc.vector.tensor_scalar(
                 out=neg_max[i][:],
-                in0=half_max[:, 0:1],
-                scalar1=half_max[:, 1:2],
+                in0=half_max[i][:, 0:1],
+                scalar1=half_max[i][:, 1:2],
                 scalar2=-SCALE,
                 op0=ALU.max,
                 op1=ALU.mult,
             )
 
         def exponent(i):
-            u, lt = i // 4, i % 4
+            f, lt = i // 4, i % 4
             if lt == 0:
-                e_sums[u] = att.tile([P, 4, 2], F32, name="e_sums%d" % u, tag="e_sums")
-            e_rows[i] = att.tile([P, TOKENS], BF16, name="e_rows%d" % i, tag="e_rows")
+                e_sums[f] = att.tile([P, 4, 2], F32, name="e_sums%d" % f, tag="e_sums")
+            e_rows[i] = att.tile([P, TOKENS], BF16, name="e_rows%d" % i, tag="e_rows", bufs=4)
             for h in range(2):
                 nc.scalar.activation(
                     out=e_rows[i][:, PASS * h : PASS * (h + 1)],
@@ -154,20 +162,20 @@ def tile_pyramidselfattentionblock_pa_t_kernel(tc, x, q, k, v_w, v_b, out):
                     func=ACT.Exp,
                     bias=neg_max[i][:, 0:1],
                     scale=SCALE,
-                    accum_out=e_sums[u][:, lt, h : h + 1],
+                    accum_out=e_sums[f][:, lt, h : h + 1],
                 )
 
-        def turn_matmuls(i):
+        def turn_e(i):
             turned[i] = psum.tile([P, 4, P], F32, name="turned%d" % i, tag="turn")
             e_words = e_rows[i][:].bitcast(F32)
             for tu in range(4):
                 nc.tensor.transpose(turned[i][:, tu, :], e_words[:, P * tu : P * (tu + 1)], ident[:])
 
-        def turn_copy(i):
-            u, lt = i // 4, i % 4
+        def group_e(i):
+            u, lt = i // 2, i % 2
             if lt == 0:
                 e_grouped[u] = att.tile(
-                    [P, 2, PASS, PACK], BF16, name="e_grouped%d" % u, tag="e_grouped", bufs=2,
+                    [P, 2, UNIT, PACK], BF16, name="e_grouped%d" % u, tag="e_grouped", bufs=2,
                     align_bytes=64,
                 )
             nc.scalar.copy(
@@ -175,60 +183,72 @@ def tile_pyramidselfattentionblock_pa_t_kernel(tc, x, q, k, v_w, v_b, out):
                 in_=turned[i][:].rearrange("p (g u) l -> p g l u", u=2),
             )
 
-        def invert_sums(u):
-            row_sum = att.tile([P, 4], F32, name="row_sum%d" % u, tag="row_sum")
-            nc.vector.tensor_reduce(out=row_sum[:], in_=e_sums[u][:], axis=AXIS_X, op=ALU.add)
-            row_inv[u] = att.tile([P, 4], F32, name="row_inv%d" % u, tag="row_inv")
-            nc.vector.reciprocal(out=row_inv[u][:], in_=row_sum[:])
-
-        def spread_inverse(u):
-            spread = psum.tile([P, PASS], F32, name="spread%d" % u, tag="turn")
-            for lt in range(4):
-                nc.tensor.transpose(
-                    spread[:, P * lt : P * (lt + 1)],
-                    row_inv[u][:, lt : lt + 1].to_broadcast([P, P]),
-                    ident[:],
-                )
-            r_cols[u] = att.tile([P, PASS], F32, name="r_cols%d" % u, tag="r_cols", bufs=4)
-            nc.scalar.copy(out=r_cols[u][:], in_=spread[:])
-
-        def quantise_e(u, tg):
-            if tg == 0:
-                e_codes[u] = att.tile([P, 2, PASS], U32, name="e_codes%d" % u, tag="e_codes", align_bytes=64)
-                e_scales[u] = att.tile([P, 2, PASS], U8, name="e_scales%d" % u, tag="e_scales", align_bytes=64)
+        def quantise_e(u):
+            e_codes[u] = att.tile(
+                [P, 2, UNIT], U32, name="e_codes%d" % u, tag="e_codes", bufs=EB, align_bytes=64
+            )
+            e_scales[u] = att.tile(
+                [P, 2, UNIT], U8, name="e_scales%d" % u, tag="e_scales", bufs=EB, align_bytes=64
+            )
             nc.vector.quantize_mx(
-                out=e_codes[u][:, tg, :].bitcast(FP8X4),
-                scales=e_scales[u][:, tg, :],
-                in_=e_grouped[u][:, tg].rearrange("p l t -> p (l t)"),
+                out=e_codes[u][:].rearrange("p g l -> p (g l)").bitcast(FP8X4),
+                scales=e_scales[u][:].rearrange("p g l -> p (g l)"),
+                in_=e_grouped[u][:].rearrange("p g l t -> p (g l t)"),
             )
 
-        def regroup_x(pair, quarter):
+        def invert_sums(f):
+            row_sum[f] = att.tile([P, 4], F32, name="row_sum%d" % f, tag="row_sum")
+            nc.vector.tensor_reduce(out=row_sum[f][:], in_=e_sums[f][:], axis=AXIS_X, op=ALU.add)
+
+        def reciprocals(f):
+            row_inv[f] = att.tile([P, 4], F32, name="row_inv%d" % f, tag="row_inv")
+            nc.vector.reciprocal(out=row_inv[f][:], in_=row_sum[f][:])
+
+        def spread_inverse(f):
+            spread[f] = psum.tile([P, PASS], F32, name="spread%d" % f, tag="turn")
+            for lt in range(4):
+                nc.tensor.transpose(
+                    spread[f][:, P * lt : P * (lt + 1)],
+                    row_inv[f][:, lt : lt + 1].to_broadcast([P, P]),
+                    ident[:],
+                )
+
+        def spread_copy(f):
+            r_cols[f] = att.tile([P, PASS], F32, name="r_cols%d" % f, tag="r_cols", bufs=4)
+            nc.scalar.copy(out=r_cols[f][:], in_=spread[f][:])
+
+        def regroup_x(pair, quarter, engine):
             w, tg = pair // 2, pair % 2
             a, d = w // 2, w % 2
             g, u = quarter // 2, quarter % 2
             grouped = xq.tile(
                 [P, 256, PACK], BF16, name="x_grouped%d%d" % (pair, quarter),
-                tag="x_grouped%d" % quarter, bufs=1, align_bytes=64,
+                tag="x_grouped%d" % quarter, bufs=XB, align_bytes=64,
             )
             x_grouped[(pair, quarter)] = grouped
-            planes = x_raw[(a, tg)][:, PACK * g : PACK * (g + 1), PASS * u : PASS * (u + 1)]
+            planes = x_raw[(a, tg)][:, PACK * g : PACK * (g + 1), SLAB * u : SLAB * (u + 1)]
             for e in range(2):
-                nc.gpsimd.tensor_scalar(
-                    out=grouped[:, P * e : P * (e + 1), :].rearrange("p (r jj) t -> p r jj t", jj=16),
-                    in0=planes.rearrange("p t (r d jj e) -> p d e r jj t", d=2, jj=16, e=2)[:, d, e],
-                    scalar1=1.0,
-                    scalar2=0.0,
-                    op0=ALU.mult,
-                    op1=ALU.add,
-                )
+                dst = grouped[:, P * e : P * (e + 1), :].rearrange("p (r jj) t -> p r jj t", jj=16)
+                src = planes.rearrange("p t (r d jj e) -> p d e r jj t", d=2, jj=16, e=2)[:, d, e]
+                if engine == "vector":
+                    nc.vector.tensor_copy(out=dst, in_=src)
+                elif engine == "scalar":
+                    nc.scalar.copy(out=dst, in_=src)
+                else:
+                    for n in range(GP // 2):
+                        rows = slice(16 // GP * n, 16 // GP * (n + 1))
+                        nc.gpsimd.tensor_scalar(
+                            out=dst[:, rows], in0=src[:, rows],
+                            scalar1=1.0, scalar2=0.0, op0=ALU.mult, op1=ALU.add,
+                        )
 
         def quantise_x(pair, quarter):
             w, tg = pair // 2, pair % 2
-            g, hh = quarter // 2, quarter % 2
-            if tg == 0 and quarter == 0:
+            g, h = quarter // 2, quarter % 2
+            if w not in x_codes:
                 x_codes[w] = xq.tile([P, 2, TOKENS], U32, name="x_codes%d" % w, tag="x_codes", align_bytes=64)
                 x_scales[w] = xq.tile([P, 2, TOKENS], U8, name="x_scales%d" % w, tag="x_scales", align_bytes=64)
-            cols = slice(PASS * tg + 256 * hh, PASS * tg + 256 * (hh + 1))
+            cols = slice(PASS * tg + 256 * h, PASS * tg + 256 * (h + 1))
             nc.vector.quantize_mx(
                 out=x_codes[w][:, g, cols].bitcast(FP8X4),
                 scales=x_scales[w][:, g, cols],
@@ -262,7 +282,7 @@ def tile_pyramidselfattentionblock_pa_t_kernel(tc, x, q, k, v_w, v_b, out):
             nc.vector.tensor_tensor(
                 out=v_grouped[pair][:, PASS * oc : PASS * (oc + 1)].rearrange("p (o t) -> p o t", t=PACK),
                 in0=v_bank[j][:].rearrange("p t o -> p o t"),
-                in1=bias_sb[:, P * oc : P * (oc + 1)].unsqueeze(2).to_broadcast([P, P, PACK]),
+                in1=bias_rows[:, P * oc : P * (oc + 1)].unsqueeze(2).to_broadcast([P, P, PACK]),
                 op=ALU.add,
             )
 
@@ -278,118 +298,256 @@ def tile_pyramidselfattentionblock_pa_t_kernel(tc, x, q, k, v_w, v_b, out):
             )
 
         def context_matmuls(j):
-            u, ot = j // 4, j % 4
-            w = u // 2
-            o_cols = slice(P * ot, P * (ot + 1))
-            c_bank[j] = psum.tile([P, PASS], F32, name="c_bank%d" % j, tag="acc")
-            for tg in range(2):
-                nc.tensor.matmul_mx(
-                    out=c_bank[j][:],
-                    lhsT=v_codes[w][:, tg, o_cols].bitcast(FP8X4),
-                    lhsT_scale=v_scales[w][:, tg, o_cols],
-                    rhs=e_codes[u][:, tg, :].bitcast(FP8X4),
-                    rhs_scale=e_scales[u][:, tg, :],
-                    start=(tg == 0),
-                    stop=(tg == 1),
-                )
+            u, half = j // 2, j % 2
+            w = u // 4
+            n = j - FLUSH
+            tag = "acc" if n < 0 else ("acc", "sim_lo", "turn", "sim_hi")[n % 4]
+            c_bank[j] = psum.tile([P, 2, UNIT], F32, name="c_bank%d" % j, tag=tag)
+            for o2 in range(2):
+                ot = 2 * half + o2
+                o_cols = slice(P * ot, P * (ot + 1))
+                for tg in range(2):
+                    nc.tensor.matmul_mx(
+                        out=c_bank[j][:, o2, :],
+                        lhsT=v_codes[w][:, tg, o_cols].bitcast(FP8X4),
+                        lhsT_scale=v_scales[w][:, tg, o_cols],
+                        rhs=e_codes[u][:, tg, :].bitcast(FP8X4),
+                        rhs_scale=e_scales[u][:, tg, :],
+                        start=(tg == 0),
+                        stop=(tg == 1),
+                    )
 
         def context_out(j):
-            u, ot = j // 4, j % 4
-            w, lh = u // 2, u % 2
+            u, half = j // 2, j % 2
+            w, slab = u // 4, u % 4
             a, d = w // 2, w % 2
             if d == 0:
-                stage[(a, lh, ot)] = ost.tile(
-                    [P, CHUNK], F32, name="stage%d%d%d" % (a, lh, ot), tag="stage%d" % ot
+                stage[(a, slab, half)] = ost.tile(
+                    [P, 2, SLAB], F32, name="stage%d%d%d" % (a, slab, half), tag="stage", align_bytes=64
                 )
-            rows = stage[(a, lh, ot)]
+            rows = stage[(a, slab, half)]
+            r_part = r_cols[u // 2][:, UNIT * (u % 2) : UNIT * (u % 2 + 1)]
             nc.vector.tensor_tensor(
-                out=rows[:].rearrange("p (i d j) -> p d i j", d=2, j=WIN)[:, d],
-                in0=c_bank[j][:].rearrange("p (i j) -> p i j", j=WIN),
-                in1=r_cols[u][:].rearrange("p (i j) -> p i j", j=WIN),
+                out=rows[:].rearrange("p o (i d j) -> p d o i j", d=2, j=WIN)[:, d],
+                in0=c_bank[j][:].rearrange("p o (i j) -> p o i j", j=WIN),
+                in1=r_part.rearrange("p (i j) -> p i j", j=WIN).unsqueeze(1).to_broadcast([P, 2, 8, WIN]),
                 op=ALU.mult,
             )
             if d == 1:
-                first = HALF_MAP * a + CHUNK * lh
+                first = HALF_MAP * a + SLAB * slab
                 nc.sync.dma_start(
-                    out=out_rows[P * ot : P * (ot + 1), first : first + CHUNK], in_=rows[:]
+                    out=out_rows[2 * P * half : 2 * P * (half + 1), first : first + SLAB].rearrange(
+                        "(t p) w -> p t w", p=P
+                    ),
+                    in_=rows[:],
                 )
 
-        def transpose_weights():
-            w_words = w_raw[:].bitcast(F32)
-            w_grouped_words = w_grouped[:].bitcast(F32)
-            for g in range(2):
-                for half in range(2):
-                    w_bank = psum.tile([P, 2, 256], F32, name="w_bank%d%d" % (g, half), tag="turn")
-                    for u in range(2):
-                        for o2 in range(2):
-                            nc.tensor.transpose(
-                                w_bank[:, u, P * o2 : P * (o2 + 1)],
-                                w_words[:, 2 * half + o2, P * (2 * g + u) : P * (2 * g + u + 1)],
-                                ident[:],
-                            )
-                    nc.scalar.copy(
-                        out=w_grouped_words[:, g, 256 * half : 256 * (half + 1), :],
-                        in_=w_bank[:].rearrange("p u o -> p o u"),
+        def transpose_weights(g, half):
+            w_words = w_raw[half][:].bitcast(F32)
+            w_bank[(g, half)] = psum.tile([P, 2, 256], F32, name="w_bank%d%d" % (g, half), tag="acc")
+            for u in range(2):
+                for o2 in range(2):
+                    nc.tensor.transpose(
+                        w_bank[(g, half)][:, u, P * o2 : P * (o2 + 1)],
+                        w_words[:, o2, P * (2 * g + u) : P * (2 * g + u + 1)],
+                        ident[:],
                     )
 
-        def quantise_weights():
-            for g in range(2):
-                nc.vector.quantize_mx(
-                    out=w_codes[:, g, :].bitcast(FP8X4),
-                    scales=w_scales[:, g, :],
-                    in_=w_grouped[:, g].rearrange("p o t -> p (o t)"),
-                )
+        def group_weights(g, half):
+            w_grouped_words = w_grouped[g][:].bitcast(F32)
+            dst = w_grouped_words[:, 256 * half : 256 * (half + 1), :]
+            src = w_bank[(g, half)][:].rearrange("p u o -> p o u")
+            if (g, half) in WSC:
+                nc.scalar.copy(out=dst, in_=src)
+            else:
+                nc.vector.tensor_copy(out=dst, in_=src)
 
-        load_qk(0)
-        load_x_chunk(0, 0)
-        nc.sync.dma_start(out=w_raw[:], in_=v_w.rearrange("(t p) c -> p t c", p=P))
-        nc.sync.dma_start(out=bias_sb[:], in_=v_b.partition_broadcast(P))
-        load_x_chunk(0, 1)
-        load_qk(1)
-        load_x_chunk(1, 0)
-        load_x_chunk(1, 1)
+        def quantise_weights(g):
+            nc.vector.quantize_mx(
+                out=w_codes[:, g, :].bitcast(FP8X4),
+                scales=w_scales[:, g, :],
+                in_=w_grouped[g][:].rearrange("p o t -> p (o t)"),
+            )
 
-        query_map(0)
+        def spread_bias():
+            bank = psum.tile([P, C_OUT], F32, name="bias_bank", tag="acc")
+            nc.tensor.matmul(out=bank[:], lhsT=ones[:], rhs=bias_row[:], start=True, stop=True)
+            nc.scalar.copy(out=bias_rows[:], in_=bank[:])
+
+        nc.vector.memset(bias_row[:], 0.0)
+        nc.vector.memset(ones[:], 1.0)
+        nc.vector.memset(warm[:], 0.0)
+        nc.scalar.activation(out=warm[:], in_=warm[:], func=ACT.Exp)
+        alloc_qk(0)
+        load_map(q_raw[0], q_rows, 0, 0, 512)
+        load_map(k_raw[0], k_rows, 0, 0, CHUNK)
+        load_map(k_raw[0], k_rows, 0, CHUNK, HALF_MAP)
+        load_map(q_raw[0], q_rows, 0, 512, HALF_MAP)
+        alloc_x(0, 0)
+        load_x(0, 0, 0)
+        load_x(0, 0, 1)
+        nc.sync.dma_start(out=bias_row[0:1, :], in_=v_b.rearrange("(c p) -> c p", c=1))
+        for half in range(2):
+            nc.sync.dma_start(
+                out=w_raw[half][:],
+                in_=v_w[2 * P * half : 2 * P * (half + 1), :].rearrange("(t p) c -> p t c", p=P),
+            )
+        load_x(0, 0, 2)
+        load_x(0, 0, 3)
+        alloc_x(0, 1)
+        for gu in range(4):
+            load_x(0, 1, gu)
+        alloc_qk(1)
+        load_map(q_raw[1], q_rows, 1, 0, HALF_MAP)
+        load_map(k_raw[1], k_rows, 1, 0, HALF_MAP)
+        for tg in range(2):
+            alloc_x(1, tg)
+            for gu in range(4):
+                load_x(1, tg, gu)
+
+        def turn_part(i):
+            turn_e(i)
+            group_e(i)
+
+        def tile_part(i):
+            half_maxima(i)
+            row_max(i)
+            exponent(i)
+
+        def rx(ns, engine):
+            for n in ns:
+                regroup_x(n // 4, n % 4, engine)
+
+        def qx(ns):
+            for n in ns:
+                quantise_x(n // 4, n % 4)
+
+        query_map(0, 0, 4)
         scores(0)
-        for quarter in range(4):
-            regroup_x(0, quarter)
-
-        for s in range(TILES + CTX_STEP):
-            block = s - VALUE_STEP
-            group = s - CTX_STEP
-            if 0 <= block < BLOCKS:
-                value_matmuls(block)
-            if 0 <= group < GROUPS:
-                context_matmuls(group)
-            if 1 <= s <= TILES:
-                turn_matmuls(s - 1)
+        scores(1)
+        tile_part(0)
+        for n in range(1, 4):
+            query_map(0, n, 4)
+        tile_part(1)
+        rx([0, 1], "vector")
+        turn_part(0)
+        scores(2)
+        tile_part(2)
+        spread_bias()
+        transpose_weights(0, 0)
+        turn_e(1)
+        scores(3)
+        qx([0, 1])
+        group_weights(0, 0)
+        transpose_weights(0, 1)
+        group_weights(0, 1)
+        tile_part(3)
+        group_e(1)
+        transpose_weights(1, 0)
+        turn_e(2)
+        scores(4)
+        group_weights(1, 0)
+        transpose_weights(1, 1)
+        group_weights(1, 1)
+        rx([2, 3], "gpsimd")
+        tile_part(4)
+        group_e(2)
+        quantise_weights(0)
+        quantise_e(0)
+        turn_e(3)
+        scores(5)
+        tile_part(5)
+        group_e(3)
+        qx([2, 3])
+        rx([4, 5], "gpsimd")
+        quantise_weights(1)
+        value_matmuls(0)
+        value_matmuls(1)
+        turn_e(4)
+        scores(6)
+        invert_sums(0)
+        tile_part(6)
+        reciprocals(0)
+        group_e(4)
+        rx([6, 7], "scalar")
+        quantise_e(1)
+        value_out(0)
+        value_out(1)
+        value_matmuls(2)
+        value_matmuls(3)
+        turn_e(5)
+        spread_inverse(0)
+        scores(7)
+        qx([4, 5])
+        rx([8, 9], "gpsimd")
+        tile_part(7)
+        group_e(5)
+        spread_copy(0)
+        query_map(1, 0, 1, "scalar")
+        value_out(2)
+        value_out(3)
+        qx([6, 7])
+        rx([10, 11], "gpsimd")
+        value_matmuls(4)
+        value_matmuls(5)
+        quantise_v(0)
+        quantise_e(2)
+        turn_e(6)
+        scores(8)
+        group_e(6)
+        value_out(4)
+        value_out(5)
+        value_matmuls(6)
+        value_matmuls(7)
+        qx([8, 9])
+        rx([12, 13], "gpsimd")
+        value_out(6)
+        value_out(7)
+        quantise_v(1)
+        qx([10, 11])
+        rx([14, 15], "gpsimd")
+        stack.enter_context(tc.manual_schedule())
+        for s in range(S0, max(CS) + 2):
+            blocks = [j for j in range(BLOCKS) if VS[j] == s]
+            vdone = [j for j in range(BLOCKS) if VS[j] == s - 1]
+            groups = [c for c in range(GROUPS) if CS[c] == s]
+            cdone = [c for c in range(GROUPS) if CS[c] == s - 1]
+            if s <= TILES:
+                turn_e(s - 1)
+            if s % 4 == 1 and 2 <= s // 4 <= TILES // 4:
+                spread_inverse(s // 4 - 1)
             if s + 1 < TILES:
                 scores(s + 1)
             if s < TILES:
+                half_maxima(s)
+            for j in vdone:
+                value_out(j)
+            if s < TILES:
                 row_max(s)
                 exponent(s)
-            if s == WEIGHT_STEP:
-                transpose_weights()
-            if 1 <= s <= TILES:
-                turn_copy(s - 1)
-            if 0 <= block < BLOCKS:
-                value_out(block)
-            if 0 <= group < GROUPS:
-                context_out(group)
-            if s % 8 == 4 and s // 8 + 1 < WINDOWS:
-                query_map(s // 8 + 1)
-            if s % 4 == 0 and 1 <= s // 4 <= UNITS:
+            if s % 4 == 0 and 2 <= s // 4 <= TILES // 4:
                 invert_sums(s // 4 - 1)
-            if s % 4 == 1 and 1 <= s // 4 <= UNITS:
-                spread_inverse(s // 4 - 1)
-            if s % 4 >= 2 and 1 <= s // 4 <= UNITS:
-                quantise_e(s // 4 - 1, s % 4 - 2)
-            if s == WEIGHT_STEP + 1:
-                quantise_weights()
-            if block % 4 == 3 and 0 <= block < BLOCKS:
-                quantise_v(block // 4)
-            x_quarter = s - X_STEP
-            if 0 <= x_quarter < 4 * PAIRS:
-                quantise_x(x_quarter // 4, x_quarter % 4)
-                if x_quarter // 4 + 1 < PAIRS:
-                    regroup_x(x_quarter // 4 + 1, x_quarter % 4)
+            for c in cdone:
+                context_out(c)
+            if s <= TILES:
+                group_e(s - 1)
+            if s % 4 == 1 and 2 <= s // 4 <= TILES // 4:
+                spread_copy(s // 4 - 1)
+            for j in blocks:
+                value_matmuls(j)
+            for c in groups:
+                context_matmuls(c)
+            if s % 8 == 4 and s // 8 + 1 < WINDOWS:
+                query_map(s // 8 + 1, 0, 1, "scalar")
+            if s % 2 == 1 and s // 2 <= UNITS:
+                quantise_e(s // 2 - 1)
+            if s % 4 == 0 and 2 <= s // 4 <= TILES // 4:
+                reciprocals(s // 4 - 1)
+            for j in vdone:
+                if j % 4 == 3:
+                    quantise_v(j // 4)
+            for n in range(4 * PAIRS):
+                if XS[n] == s:
+                    qx([n])
+                    if n >= N0 and n + 4 < 4 * PAIRS:
+                        rx([n + 4], "gpsimd")

@@ -34,10 +34,10 @@ GROUPS = 32
 SCALE = C_QK ** -0.5
 EB = 8
 XB = 1
-GP = 4
+GP = 2
 S0 = 8
 N0 = 9
-FLUSH = 23
+FLUSH = 40
 WSC = ((0, 0), (0, 1), (1, 0), (1, 1))
 VS = [-1 if j < 8 else j for j in range(BLOCKS)]
 CS = [c + 9 for c in range(GROUPS)]
@@ -289,8 +289,8 @@ def tile_pyramidselfattentionblock_pa_t_kernel(tc, x, q, k, v_w, v_b, out):
         def quantise_v(pair):
             w, tg = pair // 2, pair % 2
             if tg == 0:
-                v_codes[w] = val.tile([P, 2, C_OUT], U32, name="v_codes%d" % w, tag="v_codes", align_bytes=64)
-                v_scales[w] = val.tile([P, 2, C_OUT], U8, name="v_scales%d" % w, tag="v_scales", align_bytes=64)
+                v_codes[w] = val.tile([P, 2, C_OUT], U32, name="v_codes%d" % w, tag="v_codes", bufs=3, align_bytes=64)
+                v_scales[w] = val.tile([P, 2, C_OUT], U8, name="v_scales%d" % w, tag="v_scales", bufs=3, align_bytes=64)
             nc.vector.quantize_mx(
                 out=v_codes[w][:, tg, :].bitcast(FP8X4),
                 scales=v_scales[w][:, tg, :],
@@ -429,7 +429,7 @@ def tile_pyramidselfattentionblock_pa_t_kernel(tc, x, q, k, v_w, v_b, out):
         for n in range(1, 4):
             query_map(0, n, 4)
         tile_part(1)
-        rx([0, 1], "vector")
+        rx([0, 1], "gpsimd")
         turn_part(0)
         scores(2)
         tile_part(2)
@@ -459,7 +459,7 @@ def tile_pyramidselfattentionblock_pa_t_kernel(tc, x, q, k, v_w, v_b, out):
         tile_part(5)
         group_e(3)
         qx([2, 3])
-        rx([4, 5], "gpsimd")
+        rx([4, 5], "scalar")
         quantise_weights(1)
         value_matmuls(0)
         value_matmuls(1)
@@ -469,7 +469,7 @@ def tile_pyramidselfattentionblock_pa_t_kernel(tc, x, q, k, v_w, v_b, out):
         tile_part(6)
         reciprocals(0)
         group_e(4)
-        rx([6, 7], "scalar")
+        rx([6, 7], "vector")
         quantise_e(1)
         value_out(0)
         value_out(1)
@@ -479,7 +479,7 @@ def tile_pyramidselfattentionblock_pa_t_kernel(tc, x, q, k, v_w, v_b, out):
         spread_inverse(0)
         scores(7)
         qx([4, 5])
-        rx([8, 9], "gpsimd")
+        rx([8, 9], "scalar")
         tile_part(7)
         group_e(5)
         spread_copy(0)
@@ -487,7 +487,7 @@ def tile_pyramidselfattentionblock_pa_t_kernel(tc, x, q, k, v_w, v_b, out):
         value_out(2)
         value_out(3)
         qx([6, 7])
-        rx([10, 11], "gpsimd")
+        rx([10, 11], "scalar")
         value_matmuls(4)
         value_matmuls(5)
         quantise_v(0)
@@ -500,12 +500,14 @@ def tile_pyramidselfattentionblock_pa_t_kernel(tc, x, q, k, v_w, v_b, out):
         value_matmuls(6)
         value_matmuls(7)
         qx([8, 9])
-        rx([12, 13], "gpsimd")
+        rx([12], "gpsimd")
+        rx([13], "scalar")
         value_out(6)
         value_out(7)
         quantise_v(1)
         qx([10, 11])
-        rx([14, 15], "gpsimd")
+        rx([14], "gpsimd")
+        rx([15], "scalar")
         stack.enter_context(tc.manual_schedule())
         for s in range(S0, max(CS) + 2):
             blocks = [j for j in range(BLOCKS) if VS[j] == s]
@@ -550,4 +552,4 @@ def tile_pyramidselfattentionblock_pa_t_kernel(tc, x, q, k, v_w, v_b, out):
                 if XS[n] == s:
                     qx([n])
                     if n >= N0 and n + 4 < 4 * PAIRS:
-                        rx([n + 4], "gpsimd")
+                        rx([n + 4], "scalar" if n % 2 == 1 else "gpsimd")

@@ -36,14 +36,45 @@ EB = 8
 XB = 1
 GP = 2
 S0 = 8
+K2 = 3
 N0 = 9
-FLUSH = 40
-WSC = ((0, 0), (0, 1), (1, 0), (1, 1))
-VS = [-1 if j < 8 else j for j in range(BLOCKS)]
-CS = [c + 9 for c in range(GROUPS)]
-XS = [-1 if n < 12 else n - 4 for n in range(4 * PAIRS)]
+FLUSH = 31
+WSC = ((0, 1), (1, 1))
 
 FLOPS = 2 * C_OUT * C_IN * PIXELS + WINDOWS * 2 * TOKENS * TOKENS * (C_QK + C_OUT)
+
+
+def value_steps():
+    steps = [0] * BLOCKS
+    for j in range(8, BLOCKS):
+        fast = S0 + (j - 8) // 2
+        steps[j] = fast if fast < S0 + K2 else S0 - K2 + j - 8
+    return steps
+
+
+def context_steps(value_step):
+    first, last = S0 + K2, value_step[BLOCKS - 1]
+    order = list(range(20)) + [24, 25, 26, 27, 20, 21, 28, 29, 22, 23, 30, 31]
+    steps = [0] * GROUPS
+    now = 0
+    for n, c in enumerate(order):
+        due = first + n
+        if due > last:
+            due = last + 1 + (n - (last - first + 1)) // 2
+        now = max(now, due, 2 * (c // 2) + 4, 4 * (c // 4) + 5)
+        steps[c] = now
+    return steps
+
+
+def quantise_steps(value_step):
+    steps = [0] * (4 * PAIRS)
+    for n in range(12, 4 * PAIRS):
+        due = value_step[4 * (n // 4)]
+        if n < 20:
+            steps[n] = max(S0, due - 2) if n % 4 < 2 else due - 1
+        else:
+            steps[n] = due - 4 + n % 4
+    return steps
 
 
 def tile_pyramidselfattentionblock_pa_t_kernel(tc, x, q, k, v_w, v_b, out):
@@ -122,8 +153,9 @@ def tile_pyramidselfattentionblock_pa_t_kernel(tc, x, q, k, v_w, v_b, out):
             w, lt8 = i // 8, i % 8
             a, d = w // 2, w % 2
             keys = k_raw[a][:].rearrange("c (h i d j) -> c d h i j", h=2, d=2, j=WIN)
-            lo = psum.tile([P, PASS], F32, name="sim_lo%d" % i, tag="sim_lo")
-            hi = psum.tile([P, PASS], F32, name="sim_hi%d" % i, tag="sim_hi")
+            tags = ("acc", "acc") if i == 2 else ("sim_lo", "sim_hi")
+            lo = psum.tile([P, PASS], F32, name="sim_lo%d" % i, tag=tags[0])
+            hi = psum.tile([P, PASS], F32, name="sim_hi%d" % i, tag=tags[1])
             sim[i] = (lo, hi)
             for h in range(2):
                 nc.tensor.matmul(
@@ -300,8 +332,8 @@ def tile_pyramidselfattentionblock_pa_t_kernel(tc, x, q, k, v_w, v_b, out):
         def context_matmuls(j):
             u, half = j // 2, j % 2
             w = u // 4
-            n = j - FLUSH
-            tag = "acc" if n < 0 else ("acc", "sim_lo", "turn", "sim_hi")[n % 4]
+            late = [c for c in range(GROUPS) if CS[c] >= FLUSH]
+            tag = ("sim_lo", "sim_hi", "turn", "acc")[late.index(j) % 4] if j in late else "acc"
             c_bank[j] = psum.tile([P, 2, UNIT], F32, name="c_bank%d" % j, tag=tag)
             for o2 in range(2):
                 ot = 2 * half + o2
@@ -317,30 +349,41 @@ def tile_pyramidselfattentionblock_pa_t_kernel(tc, x, q, k, v_w, v_b, out):
                         stop=(tg == 1),
                     )
 
-        def context_out(j):
+        def context_rows(j):
             u, half = j // 2, j % 2
             w, slab = u // 4, u % 4
             a, d = w // 2, w % 2
-            if d == 0:
+            if (a, slab, half) not in stage:
                 stage[(a, slab, half)] = ost.tile(
                     [P, 2, SLAB], F32, name="stage%d%d%d" % (a, slab, half), tag="stage", align_bytes=64
                 )
-            rows = stage[(a, slab, half)]
+            return stage[(a, slab, half)][:].rearrange("p o (i d j) -> p d o i j", d=2, j=WIN)[:, d]
+
+        def context_factors(j):
+            u = j // 2
             r_part = r_cols[u // 2][:, UNIT * (u % 2) : UNIT * (u % 2 + 1)]
-            nc.vector.tensor_tensor(
-                out=rows[:].rearrange("p o (i d j) -> p d o i j", d=2, j=WIN)[:, d],
-                in0=c_bank[j][:].rearrange("p o (i j) -> p o i j", j=WIN),
-                in1=r_part.rearrange("p (i j) -> p i j", j=WIN).unsqueeze(1).to_broadcast([P, 2, 8, WIN]),
-                op=ALU.mult,
-            )
-            if d == 1:
-                first = HALF_MAP * a + SLAB * slab
+            return r_part.rearrange("p (i j) -> p i j", j=WIN).unsqueeze(1).to_broadcast([P, 2, 8, WIN])
+
+        def context_store(j):
+            u, half = j // 2, j % 2
+            w, slab = u // 4, u % 4
+            if w % 2 == 1:
+                first = HALF_MAP * (w // 2) + SLAB * slab
                 nc.sync.dma_start(
                     out=out_rows[2 * P * half : 2 * P * (half + 1), first : first + SLAB].rearrange(
                         "(t p) w -> p t w", p=P
                     ),
-                    in_=rows[:],
+                    in_=stage[(w // 2, slab, half)][:],
                 )
+
+        def context_out(j):
+            nc.vector.tensor_tensor(
+                out=context_rows(j),
+                in0=c_bank[j][:].rearrange("p o (i j) -> p o i j", j=WIN),
+                in1=context_factors(j),
+                op=ALU.mult,
+            )
+            context_store(j)
 
         def transpose_weights(g, half):
             w_words = w_raw[half][:].bitcast(F32)
@@ -374,6 +417,7 @@ def tile_pyramidselfattentionblock_pa_t_kernel(tc, x, q, k, v_w, v_b, out):
             nc.tensor.matmul(out=bank[:], lhsT=ones[:], rhs=bias_row[:], start=True, stop=True)
             nc.scalar.copy(out=bias_rows[:], in_=bank[:])
 
+        CS = context_steps(value_steps())
         nc.vector.memset(bias_row[:], 0.0)
         nc.vector.memset(ones[:], 1.0)
         nc.vector.memset(warm[:], 0.0)
@@ -428,73 +472,66 @@ def tile_pyramidselfattentionblock_pa_t_kernel(tc, x, q, k, v_w, v_b, out):
         tile_part(0)
         for n in range(1, 4):
             query_map(0, n, 4)
-        tile_part(1)
-        rx([0, 1], "gpsimd")
-        turn_part(0)
         scores(2)
-        tile_part(2)
-        spread_bias()
-        transpose_weights(0, 0)
-        turn_e(1)
+        tile_part(1)
+        rx([0], "gpsimd")
+        turn_part(0)
         scores(3)
-        qx([0, 1])
-        group_weights(0, 0)
-        transpose_weights(0, 1)
-        group_weights(0, 1)
-        tile_part(3)
-        group_e(1)
-        transpose_weights(1, 0)
-        turn_e(2)
+        tile_part(2)
+        rx([1], "gpsimd")
+        turn_part(1)
         scores(4)
-        group_weights(1, 0)
-        transpose_weights(1, 1)
-        group_weights(1, 1)
-        rx([2, 3], "gpsimd")
-        tile_part(4)
-        group_e(2)
-        quantise_weights(0)
-        quantise_e(0)
-        turn_e(3)
+        spread_bias()
+        qx([0, 1])
+        for n in range(2):
+            transpose_weights(0, n)
+            group_weights(0, n)
+        tile_part(3)
+        turn_part(2)
         scores(5)
-        tile_part(5)
-        group_e(3)
-        qx([2, 3])
-        rx([4, 5], "scalar")
+        quantise_e(0)
+        rx([2, 3], "gpsimd")
+        for n in range(2):
+            transpose_weights(1, n)
+            group_weights(1, n)
+        quantise_weights(0)
+        tile_part(4)
+        turn_part(3)
+        scores(6)
         quantise_weights(1)
+        invert_sums(0)
+        rx([4, 5], "scalar")
+        tile_part(5)
+        quantise_e(1)
+        reciprocals(0)
+        turn_part(4)
+        scores(7)
+        qx([2, 3])
         value_matmuls(0)
         value_matmuls(1)
-        turn_e(4)
-        scores(6)
-        invert_sums(0)
-        tile_part(6)
-        reciprocals(0)
-        group_e(4)
+        spread_inverse(0)
+        spread_copy(0)
         rx([6, 7], "vector")
-        quantise_e(1)
+        tile_part(6)
+        turn_part(5)
         value_out(0)
         value_out(1)
         value_matmuls(2)
         value_matmuls(3)
-        turn_e(5)
-        spread_inverse(0)
-        scores(7)
         qx([4, 5])
+        quantise_e(2)
         rx([8, 9], "scalar")
-        tile_part(7)
-        group_e(5)
-        spread_copy(0)
         query_map(1, 0, 1, "scalar")
+        scores(8)
+        tile_part(7)
+        turn_part(6)
         value_out(2)
         value_out(3)
+        quantise_v(0)
         qx([6, 7])
         rx([10, 11], "scalar")
         value_matmuls(4)
         value_matmuls(5)
-        quantise_v(0)
-        quantise_e(2)
-        turn_e(6)
-        scores(8)
-        group_e(6)
         value_out(4)
         value_out(5)
         value_matmuls(6)
@@ -502,12 +539,15 @@ def tile_pyramidselfattentionblock_pa_t_kernel(tc, x, q, k, v_w, v_b, out):
         qx([8, 9])
         rx([12], "gpsimd")
         rx([13], "scalar")
+        half_maxima(8)
         value_out(6)
         value_out(7)
         quantise_v(1)
         qx([10, 11])
         rx([14], "gpsimd")
         rx([15], "scalar")
+        VS = value_steps()
+        XS = quantise_steps(VS)
         stack.enter_context(tc.manual_schedule())
         for s in range(S0, max(CS) + 2):
             blocks = [j for j in range(BLOCKS) if VS[j] == s]
@@ -520,7 +560,7 @@ def tile_pyramidselfattentionblock_pa_t_kernel(tc, x, q, k, v_w, v_b, out):
                 spread_inverse(s // 4 - 1)
             if s + 1 < TILES:
                 scores(s + 1)
-            if s < TILES:
+            if S0 < s < TILES:
                 half_maxima(s)
             for j in vdone:
                 value_out(j)

@@ -73,7 +73,7 @@ def quantise_steps(value_step):
         if n < 20:
             steps[n] = max(S0, due - 2) if n % 4 < 2 else due - 1
         else:
-            steps[n] = due - 4 + n % 4
+            steps[n] = due - 4 + n % 4 // 2 * 2
     return steps
 
 
@@ -253,11 +253,12 @@ def tile_pyramidselfattentionblock_pa_t_kernel(tc, x, q, k, v_w, v_b, out):
             w, tg = pair // 2, pair % 2
             a, d = w // 2, w % 2
             g, u = quarter // 2, quarter % 2
-            grouped = xq.tile(
-                [P, 256, PACK], BF16, name="x_grouped%d%d" % (pair, quarter),
-                tag="x_grouped%d" % quarter, bufs=XB, align_bytes=64,
-            )
-            x_grouped[(pair, quarter)] = grouped
+            if (pair, g) not in x_grouped:
+                x_grouped[(pair, g)] = xq.tile(
+                    [P, PASS, PACK], BF16, name="x_grouped%d%d" % (pair, g),
+                    tag="x_grouped%d" % g, bufs=XB, align_bytes=64,
+                )
+            grouped = x_grouped[(pair, g)][:, 256 * u : 256 * (u + 1), :]
             planes = x_raw[(a, tg)][:, PACK * g : PACK * (g + 1), SLAB * u : SLAB * (u + 1)]
             for e in range(2):
                 dst = grouped[:, P * e : P * (e + 1), :].rearrange("p (r jj) t -> p r jj t", jj=16)
@@ -274,17 +275,16 @@ def tile_pyramidselfattentionblock_pa_t_kernel(tc, x, q, k, v_w, v_b, out):
                             scalar1=1.0, scalar2=0.0, op0=ALU.mult, op1=ALU.add,
                         )
 
-        def quantise_x(pair, quarter):
+        def quantise_x(pair, g):
             w, tg = pair // 2, pair % 2
-            g, h = quarter // 2, quarter % 2
             if w not in x_codes:
                 x_codes[w] = xq.tile([P, 2, TOKENS], U32, name="x_codes%d" % w, tag="x_codes", align_bytes=64)
                 x_scales[w] = xq.tile([P, 2, TOKENS], U8, name="x_scales%d" % w, tag="x_scales", align_bytes=64)
-            cols = slice(PASS * tg + 256 * h, PASS * tg + 256 * (h + 1))
+            cols = slice(PASS * tg, PASS * (tg + 1))
             nc.vector.quantize_mx(
                 out=x_codes[w][:, g, cols].bitcast(FP8X4),
                 scales=x_scales[w][:, g, cols],
-                in_=x_grouped[(pair, quarter)][:].rearrange("p n t -> p (n t)"),
+                in_=x_grouped[(pair, g)][:].rearrange("p n t -> p (n t)"),
             )
 
         def value_matmuls(j):
@@ -464,7 +464,8 @@ def tile_pyramidselfattentionblock_pa_t_kernel(tc, x, q, k, v_w, v_b, out):
 
         def qx(ns):
             for n in ns:
-                quantise_x(n // 4, n % 4)
+                if n % 2 == 1:
+                    quantise_x(n // 4, n % 4 // 2)
 
         query_map(0, 0, 4)
         scores(0)
@@ -588,8 +589,9 @@ def tile_pyramidselfattentionblock_pa_t_kernel(tc, x, q, k, v_w, v_b, out):
             for j in vdone:
                 if j % 4 == 3:
                     quantise_v(j // 4)
-            for n in range(4 * PAIRS):
+            for n in range(1, 4 * PAIRS, 2):
                 if XS[n] == s:
                     qx([n])
-                    if n >= N0 and n + 4 < 4 * PAIRS:
-                        rx([n + 4], "scalar" if n % 2 == 1 else "gpsimd")
+                    if n + 4 < 4 * PAIRS:
+                        rx([n + 3], "gpsimd")
+                        rx([n + 4], "scalar")

from contextlib import ExitStack

import concourse.mybir as mybir
from concourse.masks import make_identity

F32 = mybir.dt.float32
BF16 = mybir.dt.bfloat16
U32 = mybir.dt.uint32
U8 = mybir.dt.uint8
FP8X4 = mybir.dt.float8_e4m3fn_x4
ALU = mybir.AluOpType
ACT = mybir.ActivationFunctionType
AXIS_X = mybir.AxisListType.X

P = 128
PACK = 4
C_IN = 1024
C_OUT = 512
C_QK = 128
PIXELS = 4096
HALF_MAP = 2048
CHUNK = 1024
SLAB = 512
WIN = 32
TOKENS = 1024
PASS = 512
WINDOWS = 4
TILES = 32
UNIT = 256
UNITS = 16
PAIRS = 8
BLOCKS = 32
GROUPS = 32
SCALE = C_QK ** -0.5
EB = 8
XB = 1
GP = 2
S0 = 8
K2 = 3
N0 = 9
FLUSH = 31
WSC = ((0, 1), (1, 1))

FLOPS = 2 * C_OUT * C_IN * PIXELS + WINDOWS * 2 * TOKENS * TOKENS * (C_QK + C_OUT)


def value_steps():
    steps = [0] * BLOCKS
    for j in range(8, BLOCKS):
        fast = S0 + (j - 8) // 2
        steps[j] = fast if fast < S0 + K2 else S0 - K2 + j - 8
    return steps


def context_steps(value_step):
    first, last = S0 + K2, value_step[BLOCKS - 1]
    order = list(range(20)) + [24, 25, 26, 27, 20, 21, 28, 29, 22, 23, 30, 31]
    steps = [0] * GROUPS
    now = 0
    for n, c in enumerate(order):
        due = first + n
        if due > last:
            due = last + 1 + (n - (last - first + 1)) // 2
        now = max(now, due, 2 * (c // 2) + 4, 4 * (c // 4) + 5)
        steps[c] = now
    return steps


def quantise_steps(value_step):
    steps = [0] * (4 * PAIRS)
    for n in range(12, 4 * PAIRS):
        due = value_step[4 * (n // 4)]
        if n < 20:
            steps[n] = max(S0, due - 2) if n % 4 < 2 else due - 1
        else:
            steps[n] = due - 4 + n % 4 // 2 * 2
    return steps


def tile_pyramidselfattentionblock_pa_t_kernel(tc, x, q, k, v_w, v_b, out):
    nc = tc.nc
    x_rows = x.rearrange("b c h w -> (b c) (h w)")
    q_rows = q.rearrange("b c h w -> (b c) (h w)")
    k_rows = k.rearrange("b c h w -> (b c) (h w)")
    out_rows = out.rearrange("b o h w -> (b o) (h w)")

    with ExitStack() as stack:
        keep = stack.enter_context(tc.tile_pool(name="keep", bufs=1))
        maps = stack.enter_context(tc.tile_pool(name="maps", bufs=2))
        xq = stack.enter_context(tc.tile_pool(name="xq", bufs=2))
        val = stack.enter_context(tc.tile_pool(name="val", bufs=2))
        att = stack.enter_context(tc.tile_pool(name="att", bufs=3))
        ost = stack.enter_context(tc.tile_pool(name="ost", bufs=8))
        psum = stack.enter_context(tc.psum_pool(name="psum", bufs=2))

        ident = keep.tile([P, P], F32, name="ident")
        make_identity(nc, ident[:])
        bias_row = keep.tile([P, C_OUT], BF16, name="bias_row")
        bias_rows = keep.tile([P, C_OUT], F32, name="bias_rows")
        ones = keep.tile([P, P], BF16, name="ones")
        warm = keep.tile([P, 1], F32, name="warm")
        w_codes = keep.tile([P, 2, C_OUT], U32, name="w_codes", align_bytes=64)
        w_scales = keep.tile([P, 2, C_OUT], U8, name="w_scales", align_bytes=64)

        q_raw, k_raw, x_raw, q_win = {}, {}, {}, {}
        x_grouped, x_codes, x_scales = {}, {}, {}
        v_bank, v_chan, v_turned, v_grouped, v_codes, v_scales = {}, {}, {}, {}, {}, {}
        sim, half_max, neg_max, e_rows, turned, e_sums = {}, {}, {}, {}, {}, {}
        e_grouped, e_codes, e_scales, row_inv, r_cols = {}, {}, {}, {}, {}
        c_bank, stage, spread, row_sum = {}, {}, {}, {}
        w_raw, w_grouped, w_bank = {}, {}, {}
        for half in range(2):
            w_raw[half] = ost.tile([P, 2, C_IN], BF16, name="w_raw%d" % half, tag="stage", align_bytes=64)
        for g in range(2):
            w_grouped[g] = ost.tile([P, C_OUT, PACK], BF16, name="w_grouped%d" % g, tag="stage", align_bytes=64)

        def alloc_qk(a):
            q_raw[a] = maps.tile([P, HALF_MAP], BF16, name="q_raw%d" % a, tag="q_raw")
            k_raw[a] = maps.tile([P, HALF_MAP], BF16, name="k_raw%d" % a, tag="k_raw")

        def load_map(dst, rows, a, lo, hi):
            nc.sync.dma_start(out=dst[:, lo:hi], in_=rows[:, HALF_MAP * a + lo : HALF_MAP * a + hi])

        def alloc_x(a, tg):
            x_raw[(a, tg)] = maps.tile(
                [P, 8, CHUNK], BF16, name="x_raw%d%d" % (a, tg), tag="x_raw", bufs=4
            )

        def load_x(a, tg, gu):
            first = HALF_MAP * a + CHUNK * tg
            nc.sync.dma_start(
                out=x_raw[(a, tg)][:, 2 * gu : 2 * gu + 2, :],
                in_=x_rows[256 * gu : 256 * (gu + 1), first : first + CHUNK].rearrange(
                    "(p e) w -> p e w", e=2
                ),
            )

        def query_map(w, part, parts, engine="vector"):
            a, d = w // 2, w % 2
            if part == 0:
                q_win[w] = maps.tile([P, TOKENS], BF16, name="q_win%d" % w, tag="q_win")
            n = TOKENS // parts
            dst = q_win[w][:, n * part : n * (part + 1)].rearrange("c (i j) -> c i j", j=WIN)
            src = q_raw[a][:, 2 * n * part : 2 * n * (part + 1)].rearrange(
                "c (i d j) -> c d i j", d=2, j=WIN
            )[:, d]
            if engine == "scalar":
                nc.scalar.copy(out=dst, in_=src)
            else:
                nc.vector.tensor_copy(out=dst, in_=src)

        def scores(i):
            w, lt8 = i // 8, i % 8
            a, d = w // 2, w % 2
            keys = k_raw[a][:].rearrange("c (h i d j) -> c d h i j", h=2, d=2, j=WIN)
            tags = ("acc", "acc") if i == 2 else ("sim_lo", "sim_hi")
            lo = psum.tile([P, PASS], F32, name="sim_lo%d" % i, tag=tags[0])
            hi = psum.tile([P, PASS], F32, name="sim_hi%d" % i, tag=tags[1])
            sim[i] = (lo, hi)
            for h in range(2):
                nc.tensor.matmul(
                    out=sim[i][h][:].rearrange("p (i j) -> p i j", j=WIN),
                    lhsT=q_win[w][:, P * lt8 : P * (lt8 + 1)],
                    rhs=keys[:, d, h],
                    start=True,
                    stop=True,
                )

        def half_maxima(i):
            half_max[i] = att.tile([P, 2], F32, name="half_max%d" % i, tag="half_max")
            for h in range(2):
                nc.vector.reduce_max(out=half_max[i][:, h : h + 1], in_=sim[i][h][:], axis=AXIS_X)

        def row_max(i):
            neg_max[i] = att.tile([P, 1], F32, name="neg_max%d" % i, tag="neg_max")
            nc.vector.tensor_scalar(
                out=neg_max[i][:],
                in0=half_max[i][:, 0:1],
                scalar1=half_max[i][:, 1:2],
                scalar2=-SCALE,
                op0=ALU.max,
                op1=ALU.mult,
            )

        def exponent(i):
            f, lt = i // 4, i % 4
            if lt == 0:
                e_sums[f] = att.tile([P, 4, 2], F32, name="e_sums%d" % f, tag="e_sums")
            e_rows[i] = att.tile([P, TOKENS], BF16, name="e_rows%d" % i, tag="e_rows", bufs=4)
            for h in range(2):
                nc.scalar.activation(
                    out=e_rows[i][:, PASS * h : PASS * (h + 1)],
                    in_=sim[i][h][:],
                    func=ACT.Exp,
                    bias=neg_max[i][:, 0:1],
                    scale=SCALE,
                    accum_out=e_sums[f][:, lt, h : h + 1],
                )

        def turn_e(i):
            turned[i] = psum.tile([P, 4, P], F32, name="turned%d" % i, tag="turn")
            e_words = e_rows[i][:].bitcast(F32)
            for tu in range(4):
                nc.tensor.transpose(turned[i][:, tu, :], e_words[:, P * tu : P * (tu + 1)], ident[:])

        def group_e(i):
            u, lt = i // 2, i % 2
            if lt == 0:
                e_grouped[u] = att.tile(
                    [P, 2, UNIT, PACK], BF16, name="e_grouped%d" % u, tag="e_grouped", bufs=2,
                    align_bytes=64,
                )
            nc.scalar.copy(
                out=e_grouped[u][:].bitcast(F32)[:, :, P * lt : P * (lt + 1), :],
                in_=turned[i][:].rearrange("p (g u) l -> p g l u", u=2),
            )

        def quantise_e(u):
            e_codes[u] = att.tile(
                [P, 2, UNIT], U32, name="e_codes%d" % u, tag="e_codes", bufs=EB, align_bytes=64
            )
            e_scales[u] = att.tile(
                [P, 2, UNIT], U8, name="e_scales%d" % u, tag="e_scales", bufs=EB, align_bytes=64
            )
            nc.vector.quantize_mx(
                out=e_codes[u][:].rearrange("p g l -> p (g l)").bitcast(FP8X4),
                scales=e_scales[u][:].rearrange("p g l -> p (g l)"),
                in_=e_grouped[u][:].rearrange("p g l t -> p (g l t)"),
            )

        def invert_sums(f):
            row_sum[f] = att.tile([P, 4], F32, name="row_sum%d" % f, tag="row_sum")
            nc.vector.tensor_reduce(out=row_sum[f][:], in_=e_sums[f][:], axis=AXIS_X, op=ALU.add)

        def reciprocals(f):
            row_inv[f] = att.tile([P, 4], F32, name="row_inv%d" % f, tag="row_inv")
            nc.vector.reciprocal(out=row_inv[f][:], in_=row_sum[f][:])

        def spread_inverse(f):
            spread[f] = psum.tile([P, PASS], F32, name="spread%d" % f, tag="turn")
            for lt in range(4):
                nc.tensor.transpose(
                    spread[f][:, P * lt : P * (lt + 1)],
                    row_inv[f][:, lt : lt + 1].to_broadcast([P, P]),
                    ident[:],
                )

        def spread_copy(f):
            r_cols[f] = att.tile([P, PASS], F32, name="r_cols%d" % f, tag="r_cols", bufs=4)
            nc.scalar.copy(out=r_cols[f][:], in_=spread[f][:])

        def regroup_x(pair, quarter, engine):
            w, tg = pair // 2, pair % 2
            a, d = w // 2, w % 2
            g, u = quarter // 2, quarter % 2
            if (pair, g) not in x_grouped:
                x_grouped[(pair, g)] = xq.tile(
                    [P, PASS, PACK], BF16, name="x_grouped%d%d" % (pair, g),
                    tag="x_grouped%d" % g, bufs=XB, align_bytes=64,
                )
            grouped = x_grouped[(pair, g)][:, 256 * u : 256 * (u + 1), :]
            planes = x_raw[(a, tg)][:, PACK * g : PACK * (g + 1), SLAB * u : SLAB * (u + 1)]
            for e in range(2):
                dst = grouped[:, P * e : P * (e + 1), :].rearrange("p (r jj) t -> p r jj t", jj=16)
                src = planes.rearrange("p t (r d jj e) -> p d e r jj t", d=2, jj=16, e=2)[:, d, e]
                if engine == "vector":
                    nc.vector.tensor_copy(out=dst, in_=src)
                elif engine == "scalar":
                    nc.scalar.copy(out=dst, in_=src)
                else:
                    for n in range(GP // 2):
                        rows = slice(16 // GP * n, 16 // GP * (n + 1))
                        nc.gpsimd.tensor_scalar(
                            out=dst[:, rows], in0=src[:, rows],
                            scalar1=1.0, scalar2=0.0, op0=ALU.mult, op1=ALU.add,
                        )

        def quantise_x(pair, g):
            w, tg = pair // 2, pair % 2
            if w not in x_codes:
                x_codes[w] = xq.tile([P, 2, TOKENS], U32, name="x_codes%d" % w, tag="x_codes", align_bytes=64)
                x_scales[w] = xq.tile([P, 2, TOKENS], U8, name="x_scales%d" % w, tag="x_scales", align_bytes=64)
            cols = slice(PASS * tg, PASS * (tg + 1))
            nc.vector.quantize_mx(
                out=x_codes[w][:, g, cols].bitcast(FP8X4),
                scales=x_scales[w][:, g, cols],
                in_=x_grouped[(pair, g)][:].rearrange("p n t -> p (n t)"),
            )

        def value_matmuls(j):
            pair, oc = j // 4, j % 4
            w, tg = pair // 2, pair % 2
            o_cols = slice(P * oc, P * (oc + 1))
            v_bank[j] = psum.tile([P, PACK, P], F32, name="v_bank%d" % j, tag="acc")
            for t in range(PACK):
                tok = slice(PASS * tg + P * t, PASS * tg + P * (t + 1))
                for g in range(2):
                    nc.tensor.matmul_mx(
                        out=v_bank[j][:, t, :],
                        lhsT=x_codes[w][:, g, tok].bitcast(FP8X4),
                        lhsT_scale=x_scales[w][:, g, tok],
                        rhs=w_codes[:, g, o_cols].bitcast(FP8X4),
                        rhs_scale=w_scales[:, g, o_cols],
                        start=(g == 0),
                        stop=(g == 1),
                    )

        def value_out(j):
            pair, oc = j // 4, j % 4
            if oc == 0:
                v_grouped[pair] = val.tile(
                    [P, C_OUT * PACK], BF16, name="v_grouped%d" % pair, tag="v_grouped", align_bytes=64
                )
            nc.vector.tensor_tensor(
                out=v_grouped[pair][:, PASS * oc : PASS * (oc + 1)].rearrange("p (o t) -> p o t", t=PACK),
                in0=v_bank[j][:].rearrange("p t o -> p o t"),
                in1=bias_rows[:, P * oc : P * (oc + 1)].unsqueeze(2).to_broadcast([P, P, PACK]),
                op=ALU.add,
            )

        def quantise_v(pair):
            w, tg = pair // 2, pair % 2
            if tg == 0:
                v_codes[w] = val.tile([P, 2, C_OUT], U32, name="v_codes%d" % w, tag="v_codes", bufs=3, align_bytes=64)
                v_scales[w] = val.tile([P, 2, C_OUT], U8, name="v_scales%d" % w, tag="v_scales", bufs=3, align_bytes=64)
            nc.vector.quantize_mx(
                out=v_codes[w][:, tg, :].bitcast(FP8X4),
                scales=v_scales[w][:, tg, :],
                in_=v_grouped[pair][:],
            )

        def context_matmuls(j):
            u, half = j // 2, j % 2
            w = u // 4
            late = [c for c in range(GROUPS) if CS[c] >= FLUSH]
            tag = ("sim_lo", "sim_hi", "turn", "acc")[late.index(j) % 4] if j in late else "acc"
            c_bank[j] = psum.tile([P, 2, UNIT], F32, name="c_bank%d" % j, tag=tag)
            for o2 in range(2):
                ot = 2 * half + o2
                o_cols = slice(P * ot, P * (ot + 1))
                for tg in range(2):
                    nc.tensor.matmul_mx(
                        out=c_bank[j][:, o2, :],
                        lhsT=v_codes[w][:, tg, o_cols].bitcast(FP8X4),
                        lhsT_scale=v_scales[w][:, tg, o_cols],
                        rhs=e_codes[u][:, tg, :].bitcast(FP8X4),
                        rhs_scale=e_scales[u][:, tg, :],
                        start=(tg == 0),
                        stop=(tg == 1),
                    )

        def context_rows(j):
            u, half = j // 2, j % 2
            w, slab = u // 4, u % 4
            a, d = w // 2, w % 2
            if (a, slab, half) not in stage:
                stage[(a, slab, half)] = ost.tile(
                    [P, 2, SLAB], F32, name="stage%d%d%d" % (a, slab, half), tag="stage", align_bytes=64
                )
            return stage[(a, slab, half)][:].rearrange("p o (i d j) -> p d o i j", d=2, j=WIN)[:, d]

        def context_factors(j):
            u = j // 2
            r_part = r_cols[u // 2][:, UNIT * (u % 2) : UNIT * (u % 2 + 1)]
            return r_part.rearrange("p (i j) -> p i j", j=WIN).unsqueeze(1).to_broadcast([P, 2, 8, WIN])

        def context_store(j):
            u, half = j // 2, j % 2
            w, slab = u // 4, u % 4
            if w % 2 == 1:
                first = HALF_MAP * (w // 2) + SLAB * slab
                nc.sync.dma_start(
                    out=out_rows[2 * P * half : 2 * P * (half + 1), first : first + SLAB].rearrange(
                        "(t p) w -> p t w", p=P
                    ),
                    in_=stage[(w // 2, slab, half)][:],
                )

        def context_out(j):
            nc.vector.tensor_tensor(
                out=context_rows(j),
                in0=c_bank[j][:].rearrange("p o (i j) -> p o i j", j=WIN),
                in1=context_factors(j),
                op=ALU.mult,
            )
            context_store(j)

        def transpose_weights(g, half):
            w_words = w_raw[half][:].bitcast(F32)
            w_bank[(g, half)] = psum.tile([P, 2, 256], F32, name="w_bank%d%d" % (g, half), tag="acc")
            for u in range(2):
                for o2 in range(2):
                    nc.tensor.transpose(
                        w_bank[(g, half)][:, u, P * o2 : P * (o2 + 1)],
                        w_words[:, o2, P * (2 * g + u) : P * (2 * g + u + 1)],
                        ident[:],
                    )

        def group_weights(g, half):
            w_grouped_words = w_grouped[g][:].bitcast(F32)
            dst = w_grouped_words[:, 256 * half : 256 * (half + 1), :]
            src = w_bank[(g, half)][:].rearrange("p u o -> p o u")
            if (g, half) in WSC:
                nc.scalar.copy(out=dst, in_=src)
            else:
                nc.vector.tensor_copy(out=dst, in_=src)

        def quantise_weights(g):
            nc.vector.quantize_mx(
                out=w_codes[:, g, :].bitcast(FP8X4),
                scales=w_scales[:, g, :],
                in_=w_grouped[g][:].rearrange("p o t -> p (o t)"),
            )

        def spread_bias():
            bank = psum.tile([P, C_OUT], F32, name="bias_bank", tag="acc")
            nc.tensor.matmul(out=bank[:], lhsT=ones[:], rhs=bias_row[:], start=True, stop=True)
            nc.scalar.copy(out=bias_rows[:], in_=bank[:])

        CS = context_steps(value_steps())
        nc.vector.memset(bias_row[:], 0.0)
        nc.vector.memset(ones[:], 1.0)
        nc.vector.memset(warm[:], 0.0)
        nc.scalar.activation(out=warm[:], in_=warm[:], func=ACT.Exp)
        alloc_qk(0)
        load_map(q_raw[0], q_rows, 0, 0, 512)
        load_map(k_raw[0], k_rows, 0, 0, CHUNK)
        load_map(k_raw[0], k_rows, 0, CHUNK, HALF_MAP)
        load_map(q_raw[0], q_rows, 0, 512, HALF_MAP)
        alloc_x(0, 0)
        load_x(0, 0, 0)
        load_x(0, 0, 1)
        nc.sync.dma_start(out=bias_row[0:1, :], in_=v_b.rearrange("(c p) -> c p", c=1))
        for half in range(2):
            nc.sync.dma_start(
                out=w_raw[half][:],
                in_=v_w[2 * P * half : 2 * P * (half + 1), :].rearrange("(t p) c -> p t c", p=P),
            )
        load_x(0, 0, 2)
        load_x(0, 0, 3)
        alloc_x(0, 1)
        for gu in range(4):
            load_x(0, 1, gu)
        alloc_qk(1)
        load_map(q_raw[1], q_rows, 1, 0, HALF_MAP)
        load_map(k_raw[1], k_rows, 1, 0, HALF_MAP)
        for tg in range(2):
            alloc_x(1, tg)
            for gu in range(4):
                load_x(1, tg, gu)

        def turn_part(i):
            turn_e(i)
            group_e(i)

        def tile_part(i):
            half_maxima(i)
            row_max(i)
            exponent(i)

        def rx(ns, engine):
            for n in ns:
                regroup_x(n // 4, n % 4, engine)

        def qx(ns):
            for n in ns:
                if n % 2 == 1:
                    quantise_x(n // 4, n % 4 // 2)

        query_map(0, 0, 4)
        scores(0)
        scores(1)
        tile_part(0)
        for n in range(1, 4):
            query_map(0, n, 4)
        scores(2)
        tile_part(1)
        rx([0], "gpsimd")
        turn_part(0)
        scores(3)
        tile_part(2)
        rx([1], "gpsimd")
        turn_part(1)
        scores(4)
        spread_bias()
        qx([0, 1])
        for n in range(2):
            transpose_weights(0, n)
            group_weights(0, n)
        tile_part(3)
        turn_part(2)
        scores(5)
        quantise_e(0)
        rx([2, 3], "gpsimd")
        for n in range(2):
            transpose_weights(1, n)
            group_weights(1, n)
        quantise_weights(0)
        tile_part(4)
        turn_part(3)
        scores(6)
        quantise_weights(1)
        invert_sums(0)
        rx([4, 5], "scalar")
        tile_part(5)
        quantise_e(1)
        reciprocals(0)
        turn_part(4)
        scores(7)
        qx([2, 3])
        value_matmuls(0)
        value_matmuls(1)
        spread_inverse(0)
        spread_copy(0)
        rx([6, 7], "vector")
        tile_part(6)
        turn_part(5)
        value_out(0)
        value_out(1)
        value_matmuls(2)
        value_matmuls(3)
        qx([4, 5])
        quantise_e(2)
        rx([8, 9], "scalar")
        query_map(1, 0, 1, "scalar")
        scores(8)
        tile_part(7)
        turn_part(6)
        value_out(2)
        value_out(3)
        quantise_v(0)
        qx([6, 7])
        rx([10, 11], "scalar")
        value_matmuls(4)
        value_matmuls(5)
        value_out(4)
        value_out(5)
        value_matmuls(6)
        value_matmuls(7)
        qx([8, 9])
        rx([12], "gpsimd")
        rx([13], "scalar")
        half_maxima(8)
        value_out(6)
        value_out(7)
        quantise_v(1)
        qx([10, 11])
        rx([14], "gpsimd")
        rx([15], "scalar")
        VS = value_steps()
        XS = quantise_steps(VS)
        stack.enter_context(tc.manual_schedule())
        for s in range(S0, max(CS) + 2):
            blocks = [j for j in range(BLOCKS) if VS[j] == s]
            vdone = [j for j in range(BLOCKS) if VS[j] == s - 1]
            groups = [c for c in range(GROUPS) if CS[c] == s]
            cdone = [c for c in range(GROUPS) if CS[c] == s - 1]
            if s <= TILES:
                turn_e(s - 1)
            if s % 4 == 1 and 2 <= s // 4 <= TILES // 4:
                spread_inverse(s // 4 - 1)
            if s + 1 < TILES:
                scores(s + 1)
            if S0 < s < TILES:
                half_maxima(s)
            for j in vdone:
                value_out(j)
            if s < TILES:
                row_max(s)
                exponent(s)
            if s % 4 == 0 and 2 <= s // 4 <= TILES // 4:
                invert_sums(s // 4 - 1)
            for c in cdone:
                context_out(c)
            if s <= TILES:
                group_e(s - 1)
            if s % 4 == 1 and 2 <= s // 4 <= TILES // 4:
                spread_copy(s // 4 - 1)
            for j in blocks:
                value_matmuls(j)
            for c in groups:
                context_matmuls(c)
            if s % 8 == 4 and s // 8 + 1 < WINDOWS:
                query_map(s // 8 + 1, 0, 1, "scalar")
            if s % 2 == 1 and s // 2 <= UNITS:
                quantise_e(s // 2 - 1)
            if s % 4 == 0 and 2 <= s // 4 <= TILES // 4:
                reciprocals(s // 4 - 1)
            for j in vdone:
                if j % 4 == 3:
                    quantise_v(j // 4)
            for n in range(1, 4 * PAIRS, 2):
                if XS[n] == s:
                    qx([n])
                    if n + 4 < 4 * PAIRS:
                        rx([n + 3], "gpsimd")
                        rx([n + 4], "scalar")
